import numpy as np
import ml_dtypes


def mxq(x, axis, fmt="e4m3"):
    dtype, down = {"e4m3": (ml_dtypes.float8_e4m3fn, 7), "e5m2": (ml_dtypes.float8_e5m2, 14)}[fmt]
    v = np.moveaxis(np.asarray(x, np.float32).astype(ml_dtypes.bfloat16).astype(np.float64), axis, -1)
    blocks = v.reshape(v.shape[:-1] + (-1, 32))
    amax = np.abs(blocks).max(-1, keepdims=True)
    byte = np.maximum(np.where(amax > 0, np.frexp(amax)[1] - 1 + 127, 0) - down, 1)
    scale = np.exp2(byte - 127.0)
    codes = (blocks / scale).astype(np.float32).astype(dtype).astype(np.float64)
    return np.moveaxis((codes * scale).reshape(v.shape), -1, axis)


WIDE = False


def mx_kscale(k):
    if not WIDE:
        return np.ones(k)
    levels = np.array([10, -10, 5, -5, 0])
    a = np.random.permutation(np.resize(levels, k // 512 * 4)).reshape(k // 512, 4)
    idx = np.arange(k)
    return np.exp2(a[idx // 512, idx % 128 // 32])


BF16 = ml_dtypes.bfloat16


def bf(x):
    return np.asarray(x, np.float32).astype(BF16)


def f64(x):
    return np.asarray(x).astype(np.float64)


B, C, H, W = 2, 1024, 32, 32
C2 = C + C


def setup_inputs():
    s = mx_kscale(C)
    return {"x": bf(np.random.standard_normal((B, C, H, W)) * s[None, :, None, None]),
            "mask": bf(np.random.random_sample((B, 1, H, W))),
            "W_kv": bf(np.random.standard_normal((C, C2)) / np.sqrt(C) / s[:, None]),
            "b_kv": bf(np.random.standard_normal(C2) * 0.3)}


def reference(x, mask, W_kv, b_kv):
    x, mask = f64(x), f64(mask)
    b, c, h, w = x.shape
    xf = np.transpose(x, (0, 2, 3, 1)).reshape(b, h * w, c)
    kv = (mxq(xf, 2, "e4m3") @ mxq(f64(W_kv), 0, "e4m3")) + f64(b_kv)
    k, v = kv[..., :c], kv[..., c:]
    k = k / np.linalg.norm(k, axis=-1, keepdims=True)
    m = np.transpose(mask, (0, 2, 3, 1)).reshape(b, h * w, 1)
    inv = 1.0 - m
    ku = k * inv
    km = k * m
    kv_know = np.sum(ku * v, axis=-2, keepdims=True)
    kv_mask = np.sum(km * v, axis=-2, keepdims=True)
    return kv_know, kv_mask

@@ -1,0 +1,251 @@
+from contextlib import ExitStack
+
+import concourse.mybir as mybir
+from concourse.masks import make_identity
+
+FLOPS = 2 * 2048 * 1024 * 2048
+
+F32 = mybir.dt.float32
+BF16 = mybir.dt.bfloat16
+U32 = mybir.dt.uint32
+U8 = mybir.dt.uint8
+FP8X4 = mybir.dt.float8_e4m3fn_x4
+ALU = mybir.AluOpType
+ACT = mybir.ActivationFunctionType
+AX = mybir.AxisListType
+
+P = 128
+PACK = 4
+G = 2
+CH = 512
+WG = 2
+
+UNITS = ['W0', 'X0', 'W1', 'W2', 'W3', 'X1', 'X2', 'X3']
+REGROUP = {'W0': 'VV', 'X0': 'SV', 'W1': 'SV', 'W2': 'SV', 'W3': 'SS', 'X1': 'SS', 'X2': 'SS', 'X3': 'SS'}
+ORDER = (
+    ("rg", "W0", 0), ("rg", "W0", 1), ("q", "W0"), ("rg", "X0", 0), ("rg", "X0", 1), ("rg", "W1", 0),
+    ("q", "X0"), ("rg", "W1", 1), ("mx", 0, 0), ("mx", 1, 0), ("rg", "W2", 0), ("q", "W1"), ("mx", 2, 0),
+    ("mx", 3, 0), ("ev", 0, 0), ("mx", 0, 1), ("ev", 1, 0), ("mx", 1, 1), ("mx", 2, 1), ("ev", 2, 0),
+    ("rg", "W3", 0), ("mx", 3, 1), ("ev", 3, 0), ("ev", 0, 1), ("ev", 1, 1), ("sq", 0), ("ev", 2, 1),
+    ("ev", 3, 1), ("sq", 1), ("rg", "W2", 1), ("q", "W2"), ("sq", 2), ("mx", 0, 2), ("sq", 3), ("mx", 1, 2),
+    ("ev", 0, 2), ("mx", 2, 2), ("ev", 1, 2), ("pr", 0, 0), ("rt", 0), ("mx", 3, 2), ("rt", 1), ("wt", 0),
+    ("rg", "W3", 1), ("wt", 1), ("ev", 2, 2), ("pr", 1, 0), ("r", 0, 0), ("ev", 3, 2), ("pr", 2, 0), ("r", 1, 0),
+    ("rg", "X1", 0), ("q", "W3"), ("pr", 3, 0), ("r", 2, 0), ("mx", 0, 3), ("mx", 1, 3), ("ev", 0, 3),
+    ("rg", "X1", 1), ("r", 3, 0), ("ev", 1, 3), ("pr", 0, 1), ("mx", 2, 3), ("mx", 3, 3), ("ev", 2, 3),
+    ("pr", 1, 1), ("ev", 3, 3), ("r", 0, 1), ("rg", "X2", 0), ("q", "X1"), ("pr", 2, 1), ("r", 1, 1),
+    ("mx", 4, 0), ("pr", 3, 1), ("rg", "X2", 1), ("r", 2, 1), ("ev", 4, 0), ("mx", 4, 1), ("mx", 4, 2),
+    ("ev", 4, 1), ("r", 3, 1), ("ev", 4, 2), ("mx", 4, 3), ("sq", 4), ("q", "X2"), ("mx", 5, 0), ("pr", 4, 0),
+    ("mx", 5, 1), ("rg", "X3", 0), ("ev", 4, 3), ("mx", 5, 2), ("mx", 5, 3), ("ev", 5, 0), ("pr", 4, 1),
+    ("mx", 6, 0), ("ev", 5, 1), ("mx", 6, 1), ("ev", 5, 2), ("sq", 5), ("mx", 6, 2), ("ev", 5, 3), ("pr", 5, 0),
+    ("mx", 6, 3), ("ev", 6, 0), ("mx", 7, 0), ("rt", 2), ("ev", 6, 1), ("rg", "X3", 1), ("pr", 5, 1),
+    ("mx", 7, 1), ("wt", 2), ("mx", 7, 2), ("ev", 6, 2), ("r", 4, 0), ("ev", 6, 3), ("pr", 6, 0), ("r", 4, 1),
+    ("ev", 7, 0), ("r", 5, 0), ("sq", 6), ("r", 5, 1), ("q", "X3"), ("pr", 6, 1), ("mx", 7, 3), ("mx", 8, 0),
+    ("ev", 7, 1), ("mx", 8, 1), ("ev", 7, 2), ("sq", 7), ("mx", 8, 2), ("ev", 7, 3), ("pr", 7, 0), ("mx", 8, 3),
+    ("ev", 8, 0), ("mx", 9, 0), ("rt", 3), ("wt", 3), ("pr", 7, 1), ("mx", 9, 1), ("ev", 8, 1), ("r", 6, 0),
+    ("ev", 8, 2), ("sq", 8), ("r", 6, 1), ("r", 7, 0), ("ev", 8, 3), ("pr", 8, 0), ("r", 7, 1), ("ev", 9, 0),
+    ("mx", 9, 2), ("ev", 9, 1), ("pr", 8, 1), ("mx", 9, 3), ("ev", 9, 2), ("mx", 10, 0), ("sq", 9), ("ev", 9, 3),
+    ("mx", 10, 1), ("pr", 9, 0), ("mx", 10, 2), ("ev", 10, 0), ("rt", 4), ("mx", 10, 3), ("wt", 4), ("pr", 9, 1),
+    ("ev", 10, 1), ("mx", 11, 0), ("ev", 10, 2), ("sq", 10), ("r", 8, 0), ("r", 8, 1), ("ev", 10, 3),
+    ("pr", 10, 0), ("r", 9, 0), ("ev", 11, 0), ("r", 9, 1), ("mx", 11, 1), ("pr", 10, 1), ("mx", 11, 2),
+    ("ev", 11, 1), ("mx", 11, 3), ("ev", 11, 2), ("sq", 11), ("mx", 12, 0), ("ev", 11, 3), ("pr", 11, 0),
+    ("mx", 12, 1), ("ev", 12, 0), ("mx", 12, 2), ("rt", 5), ("wt", 5), ("pr", 11, 1), ("mx", 12, 3),
+    ("ev", 12, 1), ("r", 10, 0), ("ev", 12, 2), ("sq", 12), ("r", 10, 1), ("r", 11, 0), ("ev", 12, 3),
+    ("pr", 12, 0), ("r", 11, 1), ("mx", 13, 0), ("pr", 12, 1), ("mx", 13, 1), ("ev", 13, 0), ("mx", 13, 2),
+    ("ev", 13, 1), ("mx", 13, 3), ("ev", 13, 2), ("sq", 13), ("mx", 14, 0), ("ev", 13, 3), ("pr", 13, 0),
+    ("mx", 14, 1), ("ev", 14, 0), ("mx", 14, 2), ("rt", 6), ("wt", 6), ("pr", 13, 1), ("mx", 14, 3),
+    ("ev", 14, 1), ("r", 12, 0), ("ev", 14, 2), ("sq", 14), ("r", 12, 1), ("r", 13, 0), ("ev", 14, 3),
+    ("pr", 14, 0), ("r", 13, 1), ("mx", 15, 0), ("pr", 14, 1), ("mx", 15, 1), ("ev", 15, 0), ("mx", 15, 2),
+    ("ev", 15, 1), ("mx", 15, 3), ("ev", 15, 2), ("sq", 15), ("ev", 15, 3), ("pr", 15, 0), ("rt", 7), ("wt", 7),
+    ("pr", 15, 1), ("r", 14, 0), ("r", 14, 1), ("r", 15, 0), ("r", 15, 1),
+)
+
+
+def tile_hydraattention_pa_kernel(tc, x, mask, W_kv, b_kv, out_0, out_1):
+    nc = tc.nc
+    with ExitStack() as ctx:
+        ctx.enter_context(tc.manual_schedule())
+        const = ctx.enter_context(tc.tile_pool(name="const", bufs=1))
+        raws = ctx.enter_context(tc.tile_pool(name="raws", bufs=8))
+        grps = ctx.enter_context(tc.tile_pool(name="grps", bufs=2))
+        kbs = ctx.enter_context(tc.tile_pool(name="kbs", bufs=12))
+        vps = ctx.enter_context(tc.tile_pool(name="vps", bufs=16))
+        junks = ctx.enter_context(tc.tile_pool(name="junks", bufs=2))
+        mm = ctx.enter_context(tc.psum_pool(name="mm", bufs=7))
+        auxp = ctx.enter_context(tc.psum_pool(name="auxp", bufs=1))
+
+        xv = x.rearrange("b (g p j) h w -> b g p j (h w)", g=G, p=P, j=PACK)
+        wv = W_kv.rearrange("(g p j) n -> g p j n", g=G, p=P, j=PACK)
+
+        bias_in = const.tile([1, 4 * CH], BF16, name="bias_in")
+        nc.scalar.dma_start(out=bias_in[:], in_=b_kv.rearrange("(o n) -> o n", o=1))
+        mask_in = const.tile([16, P], BF16, name="mask_in")
+        nc.scalar.dma_start(
+            out=mask_in[:],
+            in_=mask.rearrange("b o h w -> (b o h w)").rearrange("(r c) -> r c", c=P),
+        )
+
+        raw_of = {}
+        for unit in UNITS:
+            idx = int(unit[1])
+            raw = raws.tile([P, G, PACK, CH], BF16, name="raw")
+            for g in range(G):
+                if unit[0] == "W":
+                    src = wv[g][:, :, idx * CH:(idx + 1) * CH]
+                else:
+                    src = xv[idx // 2, g][:, :, (idx % 2) * CH:(idx % 2 + 1) * CH]
+                nc.sync.dma_start(out=raw[:, g], in_=src)
+            raw_of[unit] = raw
+
+        warm = const.tile([P, 1], F32, name="warm")
+        nc.vector.memset(warm[:], 1.0)
+        nc.scalar.sqrt(out=warm[:], in_=warm[:])
+        bias_row = const.tile([P, 4 * CH], BF16, name="bias_row")
+        nc.vector.memset(bias_row[:], 0.0)
+        mask_f = const.tile([P, P], F32, name="mask_f")
+        nc.vector.memset(mask_f[:], 0.0)
+        ones = const.tile([P, P], BF16, name="ones")
+        nc.gpsimd.memset(ones[:], 1.0)
+        ident = const.tile([P, P], F32, name="ident")
+        make_identity(nc, ident[:])
+        res = const.tile([P, P], F32, name="res")
+        nc.gpsimd.memset(res[:], 0.0)
+        nc.vector.tensor_copy(out=bias_row[0:1, :], in_=bias_in[:])
+        nc.vector.tensor_copy(out=mask_f[0:16, :], in_=mask_in[:])
+
+        biasB = const.tile([P, 4 * CH], F32, name="biasB")
+        for c in range(4):
+            ps = mm.tile([P, CH], F32, name="ps")
+            nc.tensor.matmul(out=ps[:], lhsT=ones[:], rhs=bias_row[:, c * CH:(c + 1) * CH], start=True, stop=True)
+            nc.scalar.copy(out=biasB[:, c * CH:(c + 1) * CH], in_=ps[:])
+        ps = mm.tile([P, CH], F32, name="ps")
+        nc.tensor.transpose(out=ps[:, 0:P], in_=mask_f[:], identity=ident[:])
+        mm2 = const.tile([P, 16, 2], F32, name="mm2")
+        nc.vector.tensor_scalar(out=mm2[:, :, 0], in0=ps[:, 0:16], scalar1=-1.0, scalar2=1.0, op0=ALU.mult, op1=ALU.add)
+        nc.vector.tensor_copy(out=mm2[:, :, 1], in_=ps[:, 0:16])
+
+        aux = auxp.tile([P, 256], F32, name="aux")
+
+        grp_of = {}
+        codes = {}
+        planes = {}
+        acc_of = {}
+        kb_of = {}
+        vp_of = {}
+        n2_of = {}
+        nrm_of = {}
+        w2_of = {}
+
+        def regroup(unit, g):
+            if unit not in grp_of:
+                grp = grps.tile([P, G, CH, PACK], BF16, name="grp", align_bytes=64)
+                grp_of[unit] = grp
+            dst = grp_of[unit][:, g].rearrange("p (c i) t -> p c t i", i=4)
+            src = raw_of[unit][:, g].rearrange("p t (c i) -> p c t i", i=4)
+            eng = REGROUP[unit][g]
+            if eng == "V":
+                nc.vector.tensor_copy(out=dst, in_=src)
+            elif eng == "S":
+                nc.scalar.copy(out=dst, in_=src)
+            else:
+                nc.gpsimd.tensor_scalar(out=dst, in0=src, scalar1=1.0, scalar2=0.0, op0=ALU.mult, op1=ALU.add)
+
+        def quantise(unit):
+            cd = const.tile([P, G, CH], U32, name="cd_" + unit, align_bytes=64)
+            pl = const.tile([P, G, CH], U8, name="pl_" + unit, align_bytes=64)
+            nc.vector.quantize_mx(
+                out=cd[:].rearrange("p g w -> p (g w)").bitcast(FP8X4),
+                scales=pl[:].rearrange("p g w -> p (g w)"),
+                in_=grp_of[unit][:].rearrange("p g w t -> p (g w t)"),
+            )
+            codes[unit] = cd
+            planes[unit] = pl
+
+        def mx_group(tg, c):
+            xu = "X%d" % (tg // 4)
+            wu = "W%d" % c
+            acc = mm.tile([P, CH], F32, name="ps")
+            cols = slice((tg % 4) * P, (tg % 4 + 1) * P)
+            for g in range(G):
+                nc.tensor.matmul_mx(
+                    out=acc[:],
+                    lhsT=codes[xu][:, g, cols].bitcast(FP8X4),
+                    lhsT_scale=planes[xu][:, g, cols],
+                    rhs=codes[wu][:, g, :].bitcast(FP8X4),
+                    rhs_scale=planes[wu][:, g, :],
+                    start=(g == 0),
+                    stop=(g == G - 1),
+                )
+            acc_of[(tg, c)] = acc
+
+        def evacuate(tg, c):
+            if c < 2:
+                if tg not in kb_of:
+                    kb = kbs.tile([P, 2 * CH], F32, name="kb")
+                    kb_of[tg] = kb
+                dst = kb_of[tg][:, c * CH:(c + 1) * CH]
+            else:
+                vp = vps.tile([P, CH], F32, name="vp")
+                vp_of[(tg, c - 2)] = vp
+                dst = vp[:]
+            nc.vector.tensor_tensor(out=dst, in0=acc_of[(tg, c)][:], in1=biasB[:, c * CH:(c + 1) * CH], op=ALU.add)
+
+        def square(tg):
+            i, k = divmod(tg, WG)
+            if i not in n2_of:
+                n2 = const.tile([P, WG], F32, name="n2_%d" % i)
+                n2_of[i] = n2
+            junk = junks.tile([P, 2 * CH], BF16, name="junk")
+            nc.scalar.activation(out=junk[:], in_=kb_of[tg][:], func=ACT.Square, accum_out=n2_of[i][:, k:k + 1])
+
+        def root(i):
+            nrm = const.tile([P, WG], F32, name="nrm_%d" % i)
+            nc.scalar.sqrt(out=nrm[:], in_=n2_of[i][:])
+            nrm_of[i] = nrm
+
+        def weights(i):
+            rn = const.tile([P, WG], F32, name="rn_%d" % i)
+            nc.vector.reciprocal(out=rn[:], in_=nrm_of[i][:])
+            w2 = const.tile([P, WG, 2], F32, name="w2_%d" % i)
+            nc.vector.tensor_tensor(out=w2[:], in0=mm2[:, i * WG:(i + 1) * WG, :], in1=rn[:].unsqueeze(2).to_broadcast([P, WG, 2]), op=ALU.mult)
+            w2_of[i] = w2
+
+        def product(tg, h):
+            vp = vp_of[(tg, h)]
+            nc.gpsimd.tensor_tensor(out=vp[:], in0=vp[:], in1=kb_of[tg][:, h * CH:(h + 1) * CH], op=ALU.mult)
+
+        def token_sums(tg, h):
+            b, tt = divmod(tg, 8)
+            for q in range(4):
+                col = ((b * 8 + h * 4 + q) * 8 + tt) * 2
+                nc.tensor.matmul(out=aux[:, col:col + 2], lhsT=vp_of[(tg, h)][:, q * P:(q + 1) * P], rhs=w2_of[tg // WG][:, tg % WG, :], start=True, stop=True)
+
+        for part in ORDER:
+            kind = part[0]
+            if kind == "rg":
+                regroup(part[1], int(part[2]))
+            elif kind == "q":
+                quantise(part[1])
+            elif kind == "mx":
+                mx_group(int(part[1]), int(part[2]))
+            elif kind == "ev":
+                evacuate(int(part[1]), int(part[2]))
+            elif kind == "sq":
+                square(int(part[1]))
+            elif kind == "rt":
+                root(int(part[1]))
+            elif kind == "wt":
+                weights(int(part[1]))
+            elif kind == "pr":
+                product(int(part[1]), int(part[2]))
+            elif kind == "r":
+                token_sums(int(part[1]), int(part[2]))
+
+        auxv = aux[:].rearrange("p (r t o) -> p o r t", t=8, o=2)
+        for o in range(2):
+            nc.vector.tensor_reduce(out=res[:, o * 16:(o + 1) * 16], in_=auxv[:, o], axis=AX.X, op=ALU.add)
+        pst = mm.tile([P, CH], F32, name="ps")
+        nc.tensor.transpose(out=pst[:, 0:P], in_=res[:], identity=ident[:])
+        fin = const.tile([P, P], F32, name="fin")
+        nc.vector.tensor_copy(out=fin[0:32, :], in_=pst[0:32, 0:P])
+        nc.sync.dma_start(out=out_0.rearrange("b o (j c) -> (b o j) c", c=P), in_=fin[0:16, :])
+        nc.sync.dma_start(out=out_1.rearrange("b o (j c) -> (b o j) c", c=P), in_=fin[16:32, :])

@@ -18,46 +18,21 @@ P = 128
 PACK = 4
 G = 2
 CH = 512
-WG = 2
+TILES = 16
+PAIR = 1
+NGRP = 3
+NPAD = 4
 
 UNITS = ['W0', 'X0', 'W1', 'W2', 'W3', 'X1', 'X2', 'X3']
-REGROUP = {'W0': 'VV', 'X0': 'SV', 'W1': 'SV', 'W2': 'SV', 'W3': 'SS', 'X1': 'SS', 'X2': 'SS', 'X3': 'SS'}
-ORDER = (
-    ("rg", "W0", 0), ("rg", "W0", 1), ("q", "W0"), ("rg", "X0", 0), ("rg", "X0", 1), ("rg", "W1", 0),
-    ("q", "X0"), ("rg", "W1", 1), ("mx", 0, 0), ("mx", 1, 0), ("rg", "W2", 0), ("q", "W1"), ("mx", 2, 0),
-    ("mx", 3, 0), ("ev", 0, 0), ("mx", 0, 1), ("ev", 1, 0), ("mx", 1, 1), ("mx", 2, 1), ("ev", 2, 0),
-    ("rg", "W3", 0), ("mx", 3, 1), ("ev", 3, 0), ("ev", 0, 1), ("ev", 1, 1), ("sq", 0), ("ev", 2, 1),
-    ("ev", 3, 1), ("sq", 1), ("rg", "W2", 1), ("q", "W2"), ("sq", 2), ("mx", 0, 2), ("sq", 3), ("mx", 1, 2),
-    ("ev", 0, 2), ("mx", 2, 2), ("ev", 1, 2), ("pr", 0, 0), ("rt", 0), ("mx", 3, 2), ("rt", 1), ("wt", 0),
-    ("rg", "W3", 1), ("wt", 1), ("ev", 2, 2), ("pr", 1, 0), ("r", 0, 0), ("ev", 3, 2), ("pr", 2, 0), ("r", 1, 0),
-    ("rg", "X1", 0), ("q", "W3"), ("pr", 3, 0), ("r", 2, 0), ("mx", 0, 3), ("mx", 1, 3), ("ev", 0, 3),
-    ("rg", "X1", 1), ("r", 3, 0), ("ev", 1, 3), ("pr", 0, 1), ("mx", 2, 3), ("mx", 3, 3), ("ev", 2, 3),
-    ("pr", 1, 1), ("ev", 3, 3), ("r", 0, 1), ("rg", "X2", 0), ("q", "X1"), ("pr", 2, 1), ("r", 1, 1),
-    ("mx", 4, 0), ("pr", 3, 1), ("rg", "X2", 1), ("r", 2, 1), ("ev", 4, 0), ("mx", 4, 1), ("mx", 4, 2),
-    ("ev", 4, 1), ("r", 3, 1), ("ev", 4, 2), ("mx", 4, 3), ("sq", 4), ("q", "X2"), ("mx", 5, 0), ("pr", 4, 0),
-    ("mx", 5, 1), ("rg", "X3", 0), ("ev", 4, 3), ("mx", 5, 2), ("mx", 5, 3), ("ev", 5, 0), ("pr", 4, 1),
-    ("mx", 6, 0), ("ev", 5, 1), ("mx", 6, 1), ("ev", 5, 2), ("sq", 5), ("mx", 6, 2), ("ev", 5, 3), ("pr", 5, 0),
-    ("mx", 6, 3), ("ev", 6, 0), ("mx", 7, 0), ("rt", 2), ("ev", 6, 1), ("rg", "X3", 1), ("pr", 5, 1),
-    ("mx", 7, 1), ("wt", 2), ("mx", 7, 2), ("ev", 6, 2), ("r", 4, 0), ("ev", 6, 3), ("pr", 6, 0), ("r", 4, 1),
-    ("ev", 7, 0), ("r", 5, 0), ("sq", 6), ("r", 5, 1), ("q", "X3"), ("pr", 6, 1), ("mx", 7, 3), ("mx", 8, 0),
-    ("ev", 7, 1), ("mx", 8, 1), ("ev", 7, 2), ("sq", 7), ("mx", 8, 2), ("ev", 7, 3), ("pr", 7, 0), ("mx", 8, 3),
-    ("ev", 8, 0), ("mx", 9, 0), ("rt", 3), ("wt", 3), ("pr", 7, 1), ("mx", 9, 1), ("ev", 8, 1), ("r", 6, 0),
-    ("ev", 8, 2), ("sq", 8), ("r", 6, 1), ("r", 7, 0), ("ev", 8, 3), ("pr", 8, 0), ("r", 7, 1), ("ev", 9, 0),
-    ("mx", 9, 2), ("ev", 9, 1), ("pr", 8, 1), ("mx", 9, 3), ("ev", 9, 2), ("mx", 10, 0), ("sq", 9), ("ev", 9, 3),
-    ("mx", 10, 1), ("pr", 9, 0), ("mx", 10, 2), ("ev", 10, 0), ("rt", 4), ("mx", 10, 3), ("wt", 4), ("pr", 9, 1),
-    ("ev", 10, 1), ("mx", 11, 0), ("ev", 10, 2), ("sq", 10), ("r", 8, 0), ("r", 8, 1), ("ev", 10, 3),
-    ("pr", 10, 0), ("r", 9, 0), ("ev", 11, 0), ("r", 9, 1), ("mx", 11, 1), ("pr", 10, 1), ("mx", 11, 2),
-    ("ev", 11, 1), ("mx", 11, 3), ("ev", 11, 2), ("sq", 11), ("mx", 12, 0), ("ev", 11, 3), ("pr", 11, 0),
-    ("mx", 12, 1), ("ev", 12, 0), ("mx", 12, 2), ("rt", 5), ("wt", 5), ("pr", 11, 1), ("mx", 12, 3),
-    ("ev", 12, 1), ("r", 10, 0), ("ev", 12, 2), ("sq", 12), ("r", 10, 1), ("r", 11, 0), ("ev", 12, 3),
-    ("pr", 12, 0), ("r", 11, 1), ("mx", 13, 0), ("pr", 12, 1), ("mx", 13, 1), ("ev", 13, 0), ("mx", 13, 2),
-    ("ev", 13, 1), ("mx", 13, 3), ("ev", 13, 2), ("sq", 13), ("mx", 14, 0), ("ev", 13, 3), ("pr", 13, 0),
-    ("mx", 14, 1), ("ev", 14, 0), ("mx", 14, 2), ("rt", 6), ("wt", 6), ("pr", 13, 1), ("mx", 14, 3),
-    ("ev", 14, 1), ("r", 12, 0), ("ev", 14, 2), ("sq", 14), ("r", 12, 1), ("r", 13, 0), ("ev", 14, 3),
-    ("pr", 14, 0), ("r", 13, 1), ("mx", 15, 0), ("pr", 14, 1), ("mx", 15, 1), ("ev", 15, 0), ("mx", 15, 2),
-    ("ev", 15, 1), ("mx", 15, 3), ("ev", 15, 2), ("sq", 15), ("ev", 15, 3), ("pr", 15, 0), ("rt", 7), ("wt", 7),
-    ("pr", 15, 1), ("r", 14, 0), ("r", 14, 1), ("r", 15, 0), ("r", 15, 1),
-)
+REGROUP = {'W0': 'VV', 'X0': 'VV', 'W1': 'SV', 'W2': 'SV', 'W3': 'SV', 'X1': 'SS', 'X2': 'SS', 'X3': 'SS'}
+R_LAG = 8
+W_LAG = 4
+REGROUP_LEAD = 16
+QUANT_LEAD = 6
+
+
+def arrival(bank):
+    return max(UNITS.index("X%d" % (bank[0] // 4)), UNITS.index("W%d" % bank[1]))
 
 
 def tile_hydraattention_pa_kernel(tc, x, mask, W_kv, b_kv, out_0, out_1):
@@ -66,12 +41,13 @@ def tile_hydraattention_pa_kernel(tc, x, mask, W_kv, b_kv, out_0, out_1):
         ctx.enter_context(tc.manual_schedule())
         const = ctx.enter_context(tc.tile_pool(name="const", bufs=1))
         raws = ctx.enter_context(tc.tile_pool(name="raws", bufs=8))
-        grps = ctx.enter_context(tc.tile_pool(name="grps", bufs=2))
-        kbs = ctx.enter_context(tc.tile_pool(name="kbs", bufs=12))
-        vps = ctx.enter_context(tc.tile_pool(name="vps", bufs=16))
+        grps = ctx.enter_context(tc.tile_pool(name="grps", bufs=NGRP))
+        kbs = ctx.enter_context(tc.tile_pool(name="kbs", bufs=8))
+        vps = ctx.enter_context(tc.tile_pool(name="vps", bufs=14))
         junks = ctx.enter_context(tc.tile_pool(name="junks", bufs=2))
-        mm = ctx.enter_context(tc.psum_pool(name="mm", bufs=7))
-        auxp = ctx.enter_context(tc.psum_pool(name="auxp", bufs=1))
+        mm = ctx.enter_context(tc.psum_pool(name="mm", bufs=6))
+        sums = ctx.enter_context(tc.psum_pool(name="sums", bufs=1))
+        outs = ctx.enter_context(tc.tile_pool(name="outs", bufs=2))
 
         xv = x.rearrange("b (g p j) h w -> b g p j (h w)", g=G, p=P, j=PACK)
         wv = W_kv.rearrange("(g p j) n -> g p j n", g=G, p=P, j=PACK)
@@ -107,49 +83,58 @@ def tile_hydraattention_pa_kernel(tc, x, mask, W_kv, b_kv, out_0, out_1):
         nc.gpsimd.memset(ones[:], 1.0)
         ident = const.tile([P, P], F32, name="ident")
         make_identity(nc, ident[:])
-        res = const.tile([P, P], F32, name="res")
-        nc.gpsimd.memset(res[:], 0.0)
+        wpad = []
+        for k in range(NPAD):
+            wp = const.tile([P, P], F32, name="wpad%d" % k)
+            nc.gpsimd.memset(wp[:], 0.0)
+            wpad.append(wp)
         nc.vector.tensor_copy(out=bias_row[0:1, :], in_=bias_in[:])
         nc.vector.tensor_copy(out=mask_f[0:16, :], in_=mask_in[:])
 
         biasB = const.tile([P, 4 * CH], F32, name="biasB")
+        bias_ps = []
         for c in range(4):
             ps = mm.tile([P, CH], F32, name="ps")
             nc.tensor.matmul(out=ps[:], lhsT=ones[:], rhs=bias_row[:, c * CH:(c + 1) * CH], start=True, stop=True)
-            nc.scalar.copy(out=biasB[:, c * CH:(c + 1) * CH], in_=ps[:])
+            bias_ps.append(ps)
+
+        def bias_copies():
+            for c in range(4):
+                nc.scalar.copy(out=biasB[:, c * CH:(c + 1) * CH], in_=bias_ps[c][:])
         ps = mm.tile([P, CH], F32, name="ps")
         nc.tensor.transpose(out=ps[:, 0:P], in_=mask_f[:], identity=ident[:])
-        mm2 = const.tile([P, 16, 2], F32, name="mm2")
-        nc.vector.tensor_scalar(out=mm2[:, :, 0], in0=ps[:, 0:16], scalar1=-1.0, scalar2=1.0, op0=ALU.mult, op1=ALU.add)
-        nc.vector.tensor_copy(out=mm2[:, :, 1], in_=ps[:, 0:16])
+        mm2 = const.tile([P, TILES, 2], F32, name="mm2")
 
-        aux = auxp.tile([P, 256], F32, name="aux")
+        def mask_weights():
+            nc.vector.tensor_scalar(out=mm2[:, :, 0], in0=ps[:, 0:TILES], scalar1=-1.0, scalar2=1.0, op0=ALU.mult, op1=ALU.add)
+            nc.vector.tensor_copy(out=mm2[:, :, 1], in_=ps[:, 0:TILES])
 
         grp_of = {}
         codes = {}
         planes = {}
-        acc_of = {}
         kb_of = {}
         vp_of = {}
         n2_of = {}
         nrm_of = {}
-        w2_of = {}
+        sum_of = {}
+        row_of = {}
 
-        def regroup(unit, g):
+        def regroup(unit, engine):
             if unit not in grp_of:
                 grp = grps.tile([P, G, CH, PACK], BF16, name="grp", align_bytes=64)
                 grp_of[unit] = grp
-            dst = grp_of[unit][:, g].rearrange("p (c i) t -> p c t i", i=4)
-            src = raw_of[unit][:, g].rearrange("p t (c i) -> p c t i", i=4)
-            eng = REGROUP[unit][g]
-            if eng == "V":
-                nc.vector.tensor_copy(out=dst, in_=src)
-            elif eng == "S":
-                nc.scalar.copy(out=dst, in_=src)
-            else:
-                nc.gpsimd.tensor_scalar(out=dst, in0=src, scalar1=1.0, scalar2=0.0, op0=ALU.mult, op1=ALU.add)
+            for g in range(G):
+                dst = grp_of[unit][:, g].rearrange("p (c i) t -> p c t i", i=4)
+                src = raw_of[unit][:, g].rearrange("p t (c i) -> p c t i", i=4)
+                if REGROUP[unit][g] == engine == "V":
+                    nc.vector.tensor_copy(out=dst, in_=src)
+                if REGROUP[unit][g] == "S" and engine == "S":
+                    nc.scalar.copy(out=dst, in_=src)
+                if REGROUP[unit][g] == "G" and engine == "S":
+                    nc.gpsimd.tensor_scalar(out=dst, in0=src, scalar1=1.0, scalar2=0.0, op0=ALU.mult, op1=ALU.add)
 
         def quantise(unit):
+            regroup(unit, "V")
             cd = const.tile([P, G, CH], U32, name="cd_" + unit, align_bytes=64)
             pl = const.tile([P, G, CH], U8, name="pl_" + unit, align_bytes=64)
             nc.vector.quantize_mx(
@@ -160,11 +145,11 @@ def tile_hydraattention_pa_kernel(tc, x, mask, W_kv, b_kv, out_0, out_1):
             codes[unit] = cd
             planes[unit] = pl
 
-        def mx_group(tg, c):
-            xu = "X%d" % (tg // 4)
+        def project(t, c, dst):
+            xu = "X%d" % (t // 4)
             wu = "W%d" % c
             acc = mm.tile([P, CH], F32, name="ps")
-            cols = slice((tg % 4) * P, (tg % 4 + 1) * P)
+            cols = slice((t % 4) * P, (t % 4 + 1) * P)
             for g in range(G):
                 nc.tensor.matmul_mx(
                     out=acc[:],
@@ -175,77 +160,93 @@ def tile_hydraattention_pa_kernel(tc, x, mask, W_kv, b_kv, out_0, out_1):
                     start=(g == 0),
                     stop=(g == G - 1),
                 )
-            acc_of[(tg, c)] = acc
+            nc.vector.tensor_tensor(out=dst, in0=acc[:], in1=biasB[:, c * CH:(c + 1) * CH], op=ALU.add)
 
-        def evacuate(tg, c):
-            if c < 2:
-                if tg not in kb_of:
-                    kb = kbs.tile([P, 2 * CH], F32, name="kb")
-                    kb_of[tg] = kb
-                dst = kb_of[tg][:, c * CH:(c + 1) * CH]
-            else:
-                vp = vps.tile([P, CH], F32, name="vp")
-                vp_of[(tg, c - 2)] = vp
-                dst = vp[:]
-            nc.vector.tensor_tensor(out=dst, in0=acc_of[(tg, c)][:], in1=biasB[:, c * CH:(c + 1) * CH], op=ALU.add)
-
-        def square(tg):
-            i, k = divmod(tg, WG)
-            if i not in n2_of:
-                n2 = const.tile([P, WG], F32, name="n2_%d" % i)
-                n2_of[i] = n2
-            junk = junks.tile([P, 2 * CH], BF16, name="junk")
-            nc.scalar.activation(out=junk[:], in_=kb_of[tg][:], func=ACT.Square, accum_out=n2_of[i][:, k:k + 1])
-
-        def root(i):
-            nrm = const.tile([P, WG], F32, name="nrm_%d" % i)
-            nc.scalar.sqrt(out=nrm[:], in_=n2_of[i][:])
-            nrm_of[i] = nrm
+        def keys(t, h):
+            if t not in kb_of:
+                kb = kbs.tile([P, 2 * CH], F32, name="kb")
+                kb_of[t] = kb
+            project(t, h, kb_of[t][:, h * CH:(h + 1) * CH])
+            if h == 1:
+                i, k = divmod(t, PAIR)
+                if k == 0:
+                    n2 = const.tile([P, PAIR], F32, name="n2_%d" % i)
+                    n2_of[i] = n2
+                junk = junks.tile([P, 2 * CH], BF16, name="junk")
+                nc.scalar.activation(out=junk[:], in_=kb_of[t][:], func=ACT.Square, accum_out=n2_of[i][:, k:k + 1])
+                if k == PAIR - 1:
+                    nrm = const.tile([P, PAIR], F32, name="nrm_%d" % i)
+                    nc.scalar.sqrt(out=nrm[:], in_=n2_of[i][:])
+                    nrm_of[i] = nrm
 
         def weights(i):
-            rn = const.tile([P, WG], F32, name="rn_%d" % i)
+            rn = const.tile([P, PAIR], F32, name="rn_%d" % i)
             nc.vector.reciprocal(out=rn[:], in_=nrm_of[i][:])
-            w2 = const.tile([P, WG, 2], F32, name="w2_%d" % i)
-            nc.vector.tensor_tensor(out=w2[:], in0=mm2[:, i * WG:(i + 1) * WG, :], in1=rn[:].unsqueeze(2).to_broadcast([P, WG, 2]), op=ALU.mult)
-            w2_of[i] = w2
+            for k in range(PAIR):
+                t = i * PAIR + k
+                nc.vector.tensor_scalar(out=wpad[t % NPAD][:, 0:2], in0=mm2[:, t, :], scalar1=rn[:, k:k + 1], scalar2=None, op0=ALU.mult)
 
-        def product(tg, h):
-            vp = vp_of[(tg, h)]
-            nc.gpsimd.tensor_tensor(out=vp[:], in0=vp[:], in1=kb_of[tg][:, h * CH:(h + 1) * CH], op=ALU.mult)
+        def values(t, h):
+            vp = vps.tile([P, CH], F32, name="vp")
+            vp_of[(t, h)] = vp
+            project(t, 2 + h, vp[:])
+            nc.gpsimd.tensor_tensor(out=vp[:], in0=vp[:], in1=kb_of[t][:, h * CH:(h + 1) * CH], op=ALU.mult)
 
-        def token_sums(tg, h):
-            b, tt = divmod(tg, 8)
-            for q in range(4):
-                col = ((b * 8 + h * 4 + q) * 8 + tt) * 2
-                nc.tensor.matmul(out=aux[:, col:col + 2], lhsT=vp_of[(tg, h)][:, q * P:(q + 1) * P], rhs=w2_of[tg // WG][:, tg % WG, :], start=True, stop=True)
+        def token_sums(t, h):
+            b, tt = divmod(t, 8)
+            if tt == 0:
+                acc = sums.tile([P, CH], F32, name="sum%d" % h)
+                sum_of[h] = acc
+            nc.tensor.matmul(out=sum_of[h][:], lhsT=wpad[t % NPAD][:], rhs=vp_of[(t, h)][:], start=(tt == 0), stop=(tt == 7))
+            if tt == 7:
+                if h == 0:
+                    row = outs.tile([32, 2 * CH], F32, name="row")
+                    row_of[b] = row
+                nc.scalar.copy(out=row_of[b][:, h * CH:(h + 1) * CH], in_=sum_of[h][0:32, :])
+                if h == 1:
+                    nc.sync.dma_start(out=out_0[b], in_=row_of[b][0:1, :])
+                    nc.sync.dma_start(out=out_1[b], in_=row_of[b][1:2, :])
 
-        for part in ORDER:
-            kind = part[0]
-            if kind == "rg":
-                regroup(part[1], int(part[2]))
-            elif kind == "q":
-                quantise(part[1])
-            elif kind == "mx":
-                mx_group(int(part[1]), int(part[2]))
-            elif kind == "ev":
-                evacuate(int(part[1]), int(part[2]))
-            elif kind == "sq":
-                square(int(part[1]))
-            elif kind == "rt":
-                root(int(part[1]))
-            elif kind == "wt":
-                weights(int(part[1]))
-            elif kind == "pr":
-                product(int(part[1]), int(part[2]))
-            elif kind == "r":
-                token_sums(int(part[1]), int(part[2]))
+        BANKS = sorted([(t, c) for t in range(TILES) for c in range(4)], key=arrival)
+        first_use = {}
+        for n, (t, c) in enumerate(BANKS):
+            for unit in ("X%d" % (t // 4), "W%d" % c):
+                first_use[unit] = min(first_use.get(unit, n), n)
+        early_step = {}
+        quant_step = {}
+        for k, unit in enumerate(UNITS):
+            early_step[unit] = max(first_use[unit] - REGROUP_LEAD, 0)
+            if k >= NGRP:
+                early_step[unit] = max(early_step[unit], quant_step[UNITS[k - NGRP]])
+            quant_step[unit] = max(first_use[unit] - QUANT_LEAD, early_step[unit])
 
-        auxv = aux[:].rearrange("p (r t o) -> p o r t", t=8, o=2)
-        for o in range(2):
-            nc.vector.tensor_reduce(out=res[:, o * 16:(o + 1) * 16], in_=auxv[:, o], axis=AX.X, op=ALU.add)
-        pst = mm.tile([P, CH], F32, name="ps")
-        nc.tensor.transpose(out=pst[:, 0:P], in_=res[:], identity=ident[:])
-        fin = const.tile([P, P], F32, name="fin")
-        nc.vector.tensor_copy(out=fin[0:32, :], in_=pst[0:32, 0:P])
-        nc.sync.dma_start(out=out_0.rearrange("b o (j c) -> (b o j) c", c=P), in_=fin[0:16, :])
-        nc.sync.dma_start(out=out_1.rearrange("b o (j c) -> (b o j) c", c=P), in_=fin[16:32, :])
+        weights_at = {}
+        sums_at = {}
+        weighted = []
+        for n in range(len(BANKS) + R_LAG):
+            for unit in UNITS:
+                if early_step[unit] == n:
+                    regroup(unit, "S")
+                if quant_step[unit] == n:
+                    quantise(unit)
+                if n == 0 and unit == UNITS[1]:
+                    bias_copies()
+            if n == 0:
+                mask_weights()
+            if n < len(BANKS):
+                t, c = BANKS[n]
+                if c < 2:
+                    keys(t, c)
+                    if c == 1 and t % PAIR == PAIR - 1:
+                        weights_at[n + W_LAG] = t // PAIR
+                else:
+                    values(t, c - 2)
+                    if c == 3:
+                        sums_at[n + R_LAG] = t
+            if n in weights_at:
+                weights(weights_at[n])
+                weighted.append(weights_at[n])
+            if n in sums_at:
+                assert sums_at[n] // PAIR in weighted
+                for h in range(2):
+                    token_sums(sums_at[n], h)

@@ -19,14 +19,15 @@ PACK = 4
 G = 2
 CH = 512
 TILES = 16
-PAIR = 1
 NGRP = 3
-NPAD = 4
+NPAD = 6
+SPLIT = 384
+F_LAG = 1
+FIRST_SPLIT = 0
 
 UNITS = ['W0', 'X0', 'W1', 'W2', 'W3', 'X1', 'X2', 'X3']
-REGROUP = {'W0': 'VV', 'X0': 'VV', 'W1': 'SV', 'W2': 'SV', 'W3': 'SV', 'X1': 'SS', 'X2': 'SS', 'X3': 'SS'}
+REGROUP = {'W0': 'VV', 'X0': 'VV', 'W1': 'SV', 'W2': 'SV', 'W3': 'SS', 'X1': 'SS', 'X2': 'SS', 'X3': 'SS'}
 R_LAG = 8
-W_LAG = 4
 REGROUP_LEAD = 16
 QUANT_LEAD = 6
 
@@ -43,7 +44,7 @@ def tile_hydraattention_pa_kernel(tc, x, mask, W_kv, b_kv, out_0, out_1):
         raws = ctx.enter_context(tc.tile_pool(name="raws", bufs=8))
         grps = ctx.enter_context(tc.tile_pool(name="grps", bufs=NGRP))
         kbs = ctx.enter_context(tc.tile_pool(name="kbs", bufs=8))
-        vps = ctx.enter_context(tc.tile_pool(name="vps", bufs=14))
+        vps = ctx.enter_context(tc.tile_pool(name="vps", bufs=16))
         junks = ctx.enter_context(tc.tile_pool(name="junks", bufs=2))
         mm = ctx.enter_context(tc.psum_pool(name="mm", bufs=6))
         sums = ctx.enter_context(tc.psum_pool(name="sums", bufs=1))
@@ -74,7 +75,7 @@ def tile_hydraattention_pa_kernel(tc, x, mask, W_kv, b_kv, out_0, out_1):
 
         warm = const.tile([P, 1], F32, name="warm")
         nc.vector.memset(warm[:], 1.0)
-        nc.scalar.sqrt(out=warm[:], in_=warm[:])
+        nc.scalar.activation(out=warm[:], in_=warm[:], func=ACT.Abs_reciprocal_sqrt)
         bias_row = const.tile([P, 4 * CH], BF16, name="bias_row")
         nc.vector.memset(bias_row[:], 0.0)
         mask_f = const.tile([P, P], F32, name="mask_f")
@@ -88,6 +89,17 @@ def tile_hydraattention_pa_kernel(tc, x, mask, W_kv, b_kv, out_0, out_1):
             wp = const.tile([P, P], F32, name="wpad%d" % k)
             nc.gpsimd.memset(wp[:], 0.0)
             wpad.append(wp)
+        side = []
+        for b in range(2):
+            sd = const.tile([P, 2, SPLIT], F32, name="side%d" % b)
+            nc.gpsimd.memset(sd[:], 0.0)
+            side.append(sd)
+        pick = []
+        for o in range(2):
+            pk = const.tile([P, P], F32, name="pick%d" % o)
+            nc.gpsimd.memset(pk[:], 0.0)
+            nc.gpsimd.memset(pk[:, o:o + 1], 1.0)
+            pick.append(pk)
         nc.vector.tensor_copy(out=bias_row[0:1, :], in_=bias_in[:])
         nc.vector.tensor_copy(out=mask_f[0:16, :], in_=mask_in[:])
 
@@ -114,10 +126,7 @@ def tile_hydraattention_pa_kernel(tc, x, mask, W_kv, b_kv, out_0, out_1):
         planes = {}
         kb_of = {}
         vp_of = {}
-        n2_of = {}
-        nrm_of = {}
         sum_of = {}
-        row_of = {}
 
         def regroup(unit, engine):
             if unit not in grp_of:
@@ -168,23 +177,12 @@ def tile_hydraattention_pa_kernel(tc, x, mask, W_kv, b_kv, out_0, out_1):
                 kb_of[t] = kb
             project(t, h, kb_of[t][:, h * CH:(h + 1) * CH])
             if h == 1:
-                i, k = divmod(t, PAIR)
-                if k == 0:
-                    n2 = const.tile([P, PAIR], F32, name="n2_%d" % i)
-                    n2_of[i] = n2
+                n2 = const.tile([P, 1], F32, name="n2_%d" % t)
                 junk = junks.tile([P, 2 * CH], BF16, name="junk")
-                nc.scalar.activation(out=junk[:], in_=kb_of[t][:], func=ACT.Square, accum_out=n2_of[i][:, k:k + 1])
-                if k == PAIR - 1:
-                    nrm = const.tile([P, PAIR], F32, name="nrm_%d" % i)
-                    nc.scalar.sqrt(out=nrm[:], in_=n2_of[i][:])
-                    nrm_of[i] = nrm
-
-        def weights(i):
-            rn = const.tile([P, PAIR], F32, name="rn_%d" % i)
-            nc.vector.reciprocal(out=rn[:], in_=nrm_of[i][:])
-            for k in range(PAIR):
-                t = i * PAIR + k
-                nc.vector.tensor_scalar(out=wpad[t % NPAD][:, 0:2], in0=mm2[:, t, :], scalar1=rn[:, k:k + 1], scalar2=None, op0=ALU.mult)
+                nc.scalar.activation(out=junk[:], in_=kb_of[t][:], func=ACT.Square, accum_out=n2[:])
+                rn = const.tile([P, 1], F32, name="rn_%d" % t)
+                nc.scalar.activation(out=rn[:], in_=n2[:], func=ACT.Abs_reciprocal_sqrt)
+                nc.scalar.activation(out=wpad[t % NPAD][:, 0:2], in_=mm2[:, t, :], func=ACT.Copy, scale=rn[:])
 
         def values(t, h):
             vp = vps.tile([P, CH], F32, name="vp")
@@ -192,20 +190,29 @@ def tile_hydraattention_pa_kernel(tc, x, mask, W_kv, b_kv, out_0, out_1):
             project(t, 2 + h, vp[:])
             nc.gpsimd.tensor_tensor(out=vp[:], in0=vp[:], in1=kb_of[t][:, h * CH:(h + 1) * CH], op=ALU.mult)
 
+        def side_sums(t):
+            for o in range(2):
+                nc.vector.scalar_tensor_tensor(
+                    out=side[t // 8][:, o, :], in0=vp_of[(t, 1)][:, CH - SPLIT:CH], scalar=wpad[t % NPAD][:, o:o + 1],
+                    in1=side[t // 8][:, o, :], op0=ALU.mult, op1=ALU.add,
+                )
+
         def token_sums(t, h):
             b, tt = divmod(t, 8)
             if tt == 0:
                 acc = sums.tile([P, CH], F32, name="sum%d" % h)
                 sum_of[h] = acc
-            nc.tensor.matmul(out=sum_of[h][:], lhsT=wpad[t % NPAD][:], rhs=vp_of[(t, h)][:], start=(tt == 0), stop=(tt == 7))
-            if tt == 7:
-                if h == 0:
-                    row = outs.tile([32, 2 * CH], F32, name="row")
-                    row_of[b] = row
-                nc.scalar.copy(out=row_of[b][:, h * CH:(h + 1) * CH], in_=sum_of[h][0:32, :])
-                if h == 1:
-                    nc.sync.dma_start(out=out_0[b], in_=row_of[b][0:1, :])
-                    nc.sync.dma_start(out=out_1[b], in_=row_of[b][1:2, :])
+            width = CH - SPLIT if (h == 1 and t >= FIRST_SPLIT) else CH
+            nc.tensor.matmul(out=sum_of[h][:, 0:width], lhsT=wpad[t % NPAD][:], rhs=vp_of[(t, h)][:, 0:width], start=(tt == 0), stop=(tt == 7 and h == 0))
+
+        def finish(b):
+            for o in range(2):
+                nc.tensor.matmul(out=sum_of[1][:, CH - SPLIT:CH], lhsT=pick[o][:], rhs=side[b][:, o, :], start=False, stop=(o == 1))
+            row = outs.tile([32, 2 * CH], F32, name="row")
+            for h in range(2):
+                nc.scalar.copy(out=row[:, h * CH:(h + 1) * CH], in_=sum_of[h][0:32, :])
+            nc.sync.dma_start(out=out_0[b], in_=row[0:1, :])
+            nc.sync.dma_start(out=out_1[b], in_=row[1:2, :])
 
         BANKS = sorted([(t, c) for t in range(TILES) for c in range(4)], key=arrival)
         first_use = {}
@@ -220,9 +227,8 @@ def tile_hydraattention_pa_kernel(tc, x, mask, W_kv, b_kv, out_0, out_1):
                 early_step[unit] = max(early_step[unit], quant_step[UNITS[k - NGRP]])
             quant_step[unit] = max(first_use[unit] - QUANT_LEAD, early_step[unit])
 
-        weights_at = {}
         sums_at = {}
-        weighted = []
+        finish_at = {}
         for n in range(len(BANKS) + R_LAG):
             for unit in UNITS:
                 if early_step[unit] == n:
@@ -237,16 +243,16 @@ def tile_hydraattention_pa_kernel(tc, x, mask, W_kv, b_kv, out_0, out_1):
                 t, c = BANKS[n]
                 if c < 2:
                     keys(t, c)
-                    if c == 1 and t % PAIR == PAIR - 1:
-                        weights_at[n + W_LAG] = t // PAIR
                 else:
                     values(t, c - 2)
                     if c == 3:
                         sums_at[n + R_LAG] = t
-            if n in weights_at:
-                weights(weights_at[n])
-                weighted.append(weights_at[n])
             if n in sums_at:
-                assert sums_at[n] // PAIR in weighted
+                if sums_at[n] >= FIRST_SPLIT:
+                    side_sums(sums_at[n])
                 for h in range(2):
                     token_sums(sums_at[n], h)
+                if sums_at[n] % 8 == 7:
+                    finish_at[min(n + F_LAG, len(BANKS) + R_LAG - 1)] = sums_at[n] // 8
+            if n in finish_at:
+                finish(finish_at[n])

@@ -23,6 +23,7 @@ NGRP = 3
 NPAD = 6
 SPLIT = 384
 F_LAG = 1
+PIECE = 256
 FIRST_SPLIT = 0
 
 UNITS = ['W0', 'X0', 'W1', 'W2', 'W3', 'X1', 'X2', 'X3']
@@ -188,7 +189,8 @@ def tile_hydraattention_pa_kernel(tc, x, mask, W_kv, b_kv, out_0, out_1):
             vp = vps.tile([P, CH], F32, name="vp")
             vp_of[(t, h)] = vp
             project(t, 2 + h, vp[:])
-            nc.gpsimd.tensor_tensor(out=vp[:], in0=vp[:], in1=kb_of[t][:, h * CH:(h + 1) * CH], op=ALU.mult)
+            for lo in range(0, CH, PIECE):
+                nc.gpsimd.tensor_tensor(out=vp[:, lo:lo + PIECE], in0=vp[:, lo:lo + PIECE], in1=kb_of[t][:, h * CH + lo:h * CH + lo + PIECE], op=ALU.mult)
 
         def side_sums(t):
             for o in range(2):

@@ -21,14 +21,13 @@ CH = 512
 TILES = 16
 NGRP = 3
 NPAD = 6
-SPLIT = 384
+SPLIT = 256
 F_LAG = 1
-PIECE = 256
 FIRST_SPLIT = 0
 
 UNITS = ['W0', 'X0', 'W1', 'W2', 'W3', 'X1', 'X2', 'X3']
 REGROUP = {'W0': 'VV', 'X0': 'VV', 'W1': 'SV', 'W2': 'SV', 'W3': 'SS', 'X1': 'SS', 'X2': 'SS', 'X3': 'SS'}
-R_LAG = 8
+R_LAG = 10
 REGROUP_LEAD = 16
 QUANT_LEAD = 6
 
@@ -45,7 +44,7 @@ def tile_hydraattention_pa_kernel(tc, x, mask, W_kv, b_kv, out_0, out_1):
         raws = ctx.enter_context(tc.tile_pool(name="raws", bufs=8))
         grps = ctx.enter_context(tc.tile_pool(name="grps", bufs=NGRP))
         kbs = ctx.enter_context(tc.tile_pool(name="kbs", bufs=8))
-        vps = ctx.enter_context(tc.tile_pool(name="vps", bufs=16))
+        vps = ctx.enter_context(tc.tile_pool(name="vps", bufs=8))
         junks = ctx.enter_context(tc.tile_pool(name="junks", bufs=2))
         mm = ctx.enter_context(tc.psum_pool(name="mm", bufs=6))
         sums = ctx.enter_context(tc.psum_pool(name="sums", bufs=1))
@@ -186,16 +185,17 @@ def tile_hydraattention_pa_kernel(tc, x, mask, W_kv, b_kv, out_0, out_1):
                 nc.scalar.activation(out=wpad[t % NPAD][:, 0:2], in_=mm2[:, t, :], func=ACT.Copy, scale=rn[:])
 
         def values(t, h):
-            vp = vps.tile([P, CH], F32, name="vp")
-            vp_of[(t, h)] = vp
-            project(t, 2 + h, vp[:])
-            for lo in range(0, CH, PIECE):
-                nc.gpsimd.tensor_tensor(out=vp[:, lo:lo + PIECE], in0=vp[:, lo:lo + PIECE], in1=kb_of[t][:, h * CH + lo:h * CH + lo + PIECE], op=ALU.mult)
+            if h == 0:
+                vp = vps.tile([P, 2 * CH], F32, name="vp")
+                vp_of[t] = vp
+            project(t, 2 + h, vp_of[t][:, h * CH:(h + 1) * CH])
+            if h == 1:
+                nc.gpsimd.tensor_tensor(out=vp_of[t][:], in0=vp_of[t][:], in1=kb_of[t][:], op=ALU.mult)
 
         def side_sums(t):
             for o in range(2):
                 nc.vector.scalar_tensor_tensor(
-                    out=side[t // 8][:, o, :], in0=vp_of[(t, 1)][:, CH - SPLIT:CH], scalar=wpad[t % NPAD][:, o:o + 1],
+                    out=side[t // 8][:, o, :], in0=vp_of[t][:, 2 * CH - SPLIT:2 * CH], scalar=wpad[t % NPAD][:, o:o + 1],
                     in1=side[t // 8][:, o, :], op0=ALU.mult, op1=ALU.add,
                 )
 
@@ -205,7 +205,7 @@ def tile_hydraattention_pa_kernel(tc, x, mask, W_kv, b_kv, out_0, out_1):
                 acc = sums.tile([P, CH], F32, name="sum%d" % h)
                 sum_of[h] = acc
             width = CH - SPLIT if (h == 1 and t >= FIRST_SPLIT) else CH
-            nc.tensor.matmul(out=sum_of[h][:, 0:width], lhsT=wpad[t % NPAD][:], rhs=vp_of[(t, h)][:, 0:width], start=(tt == 0), stop=(tt == 7 and h == 0))
+            nc.tensor.matmul(out=sum_of[h][:, 0:width], lhsT=wpad[t % NPAD][:], rhs=vp_of[t][:, h * CH:h * CH + width], start=(tt == 0), stop=(tt == 7 and h == 0))
 
         def finish(b):
             for o in range(2):

@@ -23,11 +23,12 @@ NGRP = 3
 NPAD = 6
 SPLIT = 256
 F_LAG = 1
+PIECE = 512
 FIRST_SPLIT = 0
 
 UNITS = ['W0', 'X0', 'W1', 'W2', 'W3', 'X1', 'X2', 'X3']
 REGROUP = {'W0': 'VV', 'X0': 'VV', 'W1': 'SV', 'W2': 'SV', 'W3': 'SS', 'X1': 'SS', 'X2': 'SS', 'X3': 'SS'}
-R_LAG = 10
+R_LAG = 8
 REGROUP_LEAD = 16
 QUANT_LEAD = 6
 
@@ -44,7 +45,7 @@ def tile_hydraattention_pa_kernel(tc, x, mask, W_kv, b_kv, out_0, out_1):
         raws = ctx.enter_context(tc.tile_pool(name="raws", bufs=8))
         grps = ctx.enter_context(tc.tile_pool(name="grps", bufs=NGRP))
         kbs = ctx.enter_context(tc.tile_pool(name="kbs", bufs=8))
-        vps = ctx.enter_context(tc.tile_pool(name="vps", bufs=8))
+        vps = ctx.enter_context(tc.tile_pool(name="vps", bufs=16))
         junks = ctx.enter_context(tc.tile_pool(name="junks", bufs=2))
         mm = ctx.enter_context(tc.psum_pool(name="mm", bufs=6))
         sums = ctx.enter_context(tc.psum_pool(name="sums", bufs=1))
@@ -185,17 +186,16 @@ def tile_hydraattention_pa_kernel(tc, x, mask, W_kv, b_kv, out_0, out_1):
                 nc.scalar.activation(out=wpad[t % NPAD][:, 0:2], in_=mm2[:, t, :], func=ACT.Copy, scale=rn[:])
 
         def values(t, h):
-            if h == 0:
-                vp = vps.tile([P, 2 * CH], F32, name="vp")
-                vp_of[t] = vp
-            project(t, 2 + h, vp_of[t][:, h * CH:(h + 1) * CH])
-            if h == 1:
-                nc.gpsimd.tensor_tensor(out=vp_of[t][:], in0=vp_of[t][:], in1=kb_of[t][:], op=ALU.mult)
+            vp = vps.tile([P, CH], F32, name="vp")
+            vp_of[(t, h)] = vp
+            project(t, 2 + h, vp[:])
+            for lo in range(0, CH, PIECE):
+                nc.gpsimd.tensor_tensor(out=vp[:, lo:lo + PIECE], in0=vp[:, lo:lo + PIECE], in1=kb_of[t][:, h * CH + lo:h * CH + lo + PIECE], op=ALU.mult)
 
         def side_sums(t):
             for o in range(2):
                 nc.vector.scalar_tensor_tensor(
-                    out=side[t // 8][:, o, :], in0=vp_of[t][:, 2 * CH - SPLIT:2 * CH], scalar=wpad[t % NPAD][:, o:o + 1],
+                    out=side[t // 8][:, o, :], in0=vp_of[(t, 1)][:, CH - SPLIT:CH], scalar=wpad[t % NPAD][:, o:o + 1],
                     in1=side[t // 8][:, o, :], op0=ALU.mult, op1=ALU.add,
                 )
 
@@ -205,7 +205,7 @@ def tile_hydraattention_pa_kernel(tc, x, mask, W_kv, b_kv, out_0, out_1):
                 acc = sums.tile([P, CH], F32, name="sum%d" % h)
                 sum_of[h] = acc
             width = CH - SPLIT if (h == 1 and t >= FIRST_SPLIT) else CH
-            nc.tensor.matmul(out=sum_of[h][:, 0:width], lhsT=wpad[t % NPAD][:], rhs=vp_of[t][:, h * CH:h * CH + width], start=(tt == 0), stop=(tt == 7 and h == 0))
+            nc.tensor.matmul(out=sum_of[h][:, 0:width], lhsT=wpad[t % NPAD][:], rhs=vp_of[(t, h)][:, 0:width], start=(tt == 0), stop=(tt == 7 and h == 0))
 
         def finish(b):
             for o in range(2):

@@ -129,11 +129,11 @@ def tile_hydraattention_pa_kernel(tc, x, mask, W_kv, b_kv, out_0, out_1):
         vp_of = {}
         sum_of = {}
 
-        def regroup(unit, engine):
+        def regroup(unit, engine, only=(0, 1)):
             if unit not in grp_of:
                 grp = grps.tile([P, G, CH, PACK], BF16, name="grp", align_bytes=64)
                 grp_of[unit] = grp
-            for g in range(G):
+            for g in only:
                 dst = grp_of[unit][:, g].rearrange("p (c i) t -> p c t i", i=4)
                 src = raw_of[unit][:, g].rearrange("p t (c i) -> p c t i", i=4)
                 if REGROUP[unit][g] == engine == "V":
@@ -143,17 +143,24 @@ def tile_hydraattention_pa_kernel(tc, x, mask, W_kv, b_kv, out_0, out_1):
                 if REGROUP[unit][g] == "G" and engine == "S":
                     nc.gpsimd.tensor_scalar(out=dst, in0=src, scalar1=1.0, scalar2=0.0, op0=ALU.mult, op1=ALU.add)
 
-        def quantise(unit):
-            regroup(unit, "V")
+        def quantise(unit, halves):
             cd = const.tile([P, G, CH], U32, name="cd_" + unit, align_bytes=64)
             pl = const.tile([P, G, CH], U8, name="pl_" + unit, align_bytes=64)
-            nc.vector.quantize_mx(
-                out=cd[:].rearrange("p g w -> p (g w)").bitcast(FP8X4),
-                scales=pl[:].rearrange("p g w -> p (g w)"),
-                in_=grp_of[unit][:].rearrange("p g w t -> p (g w t)"),
-            )
             codes[unit] = cd
             planes[unit] = pl
+            if halves:
+                for g in range(G):
+                    nc.vector.quantize_mx(
+                        out=cd[:, g, :].bitcast(FP8X4),
+                        scales=pl[:, g, :],
+                        in_=grp_of[unit][:, g].rearrange("p w t -> p (w t)"),
+                    )
+            else:
+                nc.vector.quantize_mx(
+                    out=cd[:].rearrange("p g w -> p (g w)").bitcast(FP8X4),
+                    scales=pl[:].rearrange("p g w -> p (g w)"),
+                    in_=grp_of[unit][:].rearrange("p g w t -> p (g w t)"),
+                )
 
         def project(t, c, dst):
             xu = "X%d" % (t // 4)
@@ -232,15 +239,27 @@ def tile_hydraattention_pa_kernel(tc, x, mask, W_kv, b_kv, out_0, out_1):
         sums_at = {}
         finish_at = {}
         for n in range(len(BANKS) + R_LAG):
-            for unit in UNITS:
+            for unit in UNITS[0:3]:
+                if n == 0:
+                    regroup(unit, "S")
+                    if unit == UNITS[1]:
+                        bias_copies()
+            if n == 0:
+                regroup(UNITS[0], "V")
+                regroup(UNITS[1], "V", only=(0,))
+                quantise(UNITS[0], False)
+                regroup(UNITS[1], "V", only=(1,))
+                quantise(UNITS[1], True)
+                regroup(UNITS[2], "V")
+                mask_weights()
+                quantise(UNITS[2], False)
+            for unit in UNITS[3:]:
                 if early_step[unit] == n:
                     regroup(unit, "S")
+                if quant_step[unit] == n + 1:
+                    regroup(unit, "V")
                 if quant_step[unit] == n:
-                    quantise(unit)
-                if n == 0 and unit == UNITS[1]:
-                    bias_copies()
-            if n == 0:
-                mask_weights()
+                    quantise(unit, False)
             if n < len(BANKS):
                 t, c = BANKS[n]
                 if c < 2:

@@ -27,7 +27,7 @@ PIECE = 512
 FIRST_SPLIT = 0
 
 UNITS = ['W0', 'X0', 'W1', 'W2', 'W3', 'X1', 'X2', 'X3']
-REGROUP = {'W0': 'VV', 'X0': 'VV', 'W1': 'SV', 'W2': 'SV', 'W3': 'SS', 'X1': 'SS', 'X2': 'SS', 'X3': 'SS'}
+REGROUP = {'W0': 'VV', 'X0': 'SV', 'W1': 'SV', 'W2': 'SV', 'W3': 'SS', 'X1': 'SS', 'X2': 'SS', 'X3': 'SS'}
 R_LAG = 8
 REGROUP_LEAD = 16
 QUANT_LEAD = 6
@@ -239,16 +239,14 @@ def tile_hydraattention_pa_kernel(tc, x, mask, W_kv, b_kv, out_0, out_1):
         sums_at = {}
         finish_at = {}
         for n in range(len(BANKS) + R_LAG):
-            for unit in UNITS[0:3]:
-                if n == 0:
+            if n == 0:
+                bias_copies()
+                for unit in UNITS[0:3]:
                     regroup(unit, "S")
-                    if unit == UNITS[1]:
-                        bias_copies()
             if n == 0:
                 regroup(UNITS[0], "V")
-                regroup(UNITS[1], "V", only=(0,))
-                quantise(UNITS[0], False)
-                regroup(UNITS[1], "V", only=(1,))
+                quantise(UNITS[0], True)
+                regroup(UNITS[1], "V")
                 quantise(UNITS[1], True)
                 regroup(UNITS[2], "V")
                 mask_weights()

@@ -20,17 +20,17 @@ G = 2
 CH = 512
 TILES = 16
 NGRP = 3
-NPAD = 6
-SPLIT = 256
-F_LAG = 1
-PIECE = 512
-FIRST_SPLIT = 0
-
 UNITS = ['W0', 'X0', 'W1', 'W2', 'W3', 'X1', 'X2', 'X3']
 REGROUP = {'W0': 'VV', 'X0': 'SV', 'W1': 'SV', 'W2': 'SV', 'W3': 'SS', 'X1': 'SS', 'X2': 'SS', 'X3': 'SS'}
 R_LAG = 8
+NPAD = 6
+ST = 4
+MV = 1024 - 128 * ST
+JOBS = (1, 1)
+LAST_LAG = 0
 REGROUP_LEAD = 16
 QUANT_LEAD = 6
+RAWS = 8
 
 
 def arrival(bank):
@@ -42,14 +42,14 @@ def tile_hydraattention_pa_kernel(tc, x, mask, W_kv, b_kv, out_0, out_1):
     with ExitStack() as ctx:
         ctx.enter_context(tc.manual_schedule())
         const = ctx.enter_context(tc.tile_pool(name="const", bufs=1))
-        raws = ctx.enter_context(tc.tile_pool(name="raws", bufs=8))
+        raws = ctx.enter_context(tc.tile_pool(name="raws", bufs=RAWS))
         grps = ctx.enter_context(tc.tile_pool(name="grps", bufs=NGRP))
-        kbs = ctx.enter_context(tc.tile_pool(name="kbs", bufs=8))
-        vps = ctx.enter_context(tc.tile_pool(name="vps", bufs=16))
+        kbs = ctx.enter_context(tc.tile_pool(name="kbs", bufs=6))
+        vps = ctx.enter_context(tc.tile_pool(name="vps", bufs=12))
         junks = ctx.enter_context(tc.tile_pool(name="junks", bufs=2))
         mm = ctx.enter_context(tc.psum_pool(name="mm", bufs=6))
         sums = ctx.enter_context(tc.psum_pool(name="sums", bufs=1))
-        outs = ctx.enter_context(tc.tile_pool(name="outs", bufs=2))
+        outs = ctx.enter_context(tc.tile_pool(name="outs", bufs=4))
 
         xv = x.rearrange("b (g p j) h w -> b g p j (h w)", g=G, p=P, j=PACK)
         wv = W_kv.rearrange("(g p j) n -> g p j n", g=G, p=P, j=PACK)
@@ -85,22 +85,18 @@ def tile_hydraattention_pa_kernel(tc, x, mask, W_kv, b_kv, out_0, out_1):
         nc.gpsimd.memset(ones[:], 1.0)
         ident = const.tile([P, P], F32, name="ident")
         make_identity(nc, ident[:])
+        ident16 = const.tile([P, P], BF16, name="ident16")
+        make_identity(nc, ident16[:])
         wpad = []
         for k in range(NPAD):
             wp = const.tile([P, P], F32, name="wpad%d" % k)
             nc.gpsimd.memset(wp[:], 0.0)
             wpad.append(wp)
-        side = []
+        totals = []
         for b in range(2):
-            sd = const.tile([P, 2, SPLIT], F32, name="side%d" % b)
-            nc.gpsimd.memset(sd[:], 0.0)
-            side.append(sd)
-        pick = []
-        for o in range(2):
-            pk = const.tile([P, P], F32, name="pick%d" % o)
-            nc.gpsimd.memset(pk[:], 0.0)
-            nc.gpsimd.memset(pk[:, o:o + 1], 1.0)
-            pick.append(pk)
+            tot = const.tile([P, P], F32, name="tot%d" % b)
+            nc.gpsimd.memset(tot[:], 0.0)
+            totals.append(tot)
         nc.vector.tensor_copy(out=bias_row[0:1, :], in_=bias_in[:])
         nc.vector.tensor_copy(out=mask_f[0:16, :], in_=mask_in[:])
 
@@ -128,6 +124,10 @@ def tile_hydraattention_pa_kernel(tc, x, mask, W_kv, b_kv, out_0, out_1):
         kb_of = {}
         vp_of = {}
         sum_of = {}
+        mv_of = {}
+        queue = []
+        ready_at = {}
+        step = [0]
 
         def regroup(unit, engine, only=(0, 1)):
             if unit not in grp_of:
@@ -140,8 +140,13 @@ def tile_hydraattention_pa_kernel(tc, x, mask, W_kv, b_kv, out_0, out_1):
                     nc.vector.tensor_copy(out=dst, in_=src)
                 if REGROUP[unit][g] == "S" and engine == "S":
                     nc.scalar.copy(out=dst, in_=src)
-                if REGROUP[unit][g] == "G" and engine == "S":
-                    nc.gpsimd.tensor_scalar(out=dst, in0=src, scalar1=1.0, scalar2=0.0, op0=ALU.mult, op1=ALU.add)
+                if REGROUP[unit][g] == "P" and engine == "S":
+                    for lo in range(0, CH, 256):
+                        ps2 = mm.tile([P, 4 * 256], BF16, name="ps")
+                        for q in range(2):
+                            rhs = raw_of[unit][:, g, :, lo + q * 128:lo + q * 128 + 128].rearrange("p t c -> p c t")
+                            nc.tensor.matmul(out=ps2[:, q * 512:(q + 1) * 512], lhsT=ident16[:], rhs=rhs, start=True, stop=True)
+                        nc.scalar.copy(out=grp_of[unit][:, g, lo:lo + 256].rearrange("p c t -> p (c t)"), in_=ps2[:])
 
         def quantise(unit, halves):
             cd = const.tile([P, G, CH], U32, name="cd_" + unit, align_bytes=64)
@@ -177,6 +182,8 @@ def tile_hydraattention_pa_kernel(tc, x, mask, W_kv, b_kv, out_0, out_1):
                     start=(g == 0),
                     stop=(g == G - 1),
                 )
+                for k in range(JOBS[g]):
+                    one_sum()
             nc.vector.tensor_tensor(out=dst, in0=acc[:], in1=biasB[:, c * CH:(c + 1) * CH], op=ALU.add)
 
         def keys(t, h):
@@ -184,44 +191,66 @@ def tile_hydraattention_pa_kernel(tc, x, mask, W_kv, b_kv, out_0, out_1):
                 kb = kbs.tile([P, 2 * CH], F32, name="kb")
                 kb_of[t] = kb
             project(t, h, kb_of[t][:, h * CH:(h + 1) * CH])
-            if h == 1:
-                n2 = const.tile([P, 1], F32, name="n2_%d" % t)
-                junk = junks.tile([P, 2 * CH], BF16, name="junk")
-                nc.scalar.activation(out=junk[:], in_=kb_of[t][:], func=ACT.Square, accum_out=n2[:])
-                rn = const.tile([P, 1], F32, name="rn_%d" % t)
-                nc.scalar.activation(out=rn[:], in_=n2[:], func=ACT.Abs_reciprocal_sqrt)
-                nc.scalar.activation(out=wpad[t % NPAD][:, 0:2], in_=mm2[:, t, :], func=ACT.Copy, scale=rn[:])
+
+        def weights(t):
+            n2 = const.tile([P, 1], F32, name="n2_%d" % t)
+            junk = junks.tile([P, 2 * CH], BF16, name="junk")
+            nc.scalar.activation(out=junk[:], in_=kb_of[t][:], func=ACT.Square, accum_out=n2[:])
+            rn = const.tile([P, 1], F32, name="rn_%d" % t)
+            nc.scalar.activation(out=rn[:], in_=n2[:], func=ACT.Abs_reciprocal_sqrt)
+            nc.scalar.activation(out=wpad[t % NPAD][:, 0:2], in_=mm2[:, t, :], func=ACT.Copy, scale=rn[:])
 
         def values(t, h):
             vp = vps.tile([P, CH], F32, name="vp")
             vp_of[(t, h)] = vp
             project(t, 2 + h, vp[:])
-            for lo in range(0, CH, PIECE):
-                nc.gpsimd.tensor_tensor(out=vp[:, lo:lo + PIECE], in0=vp[:, lo:lo + PIECE], in1=kb_of[t][:, h * CH + lo:h * CH + lo + PIECE], op=ALU.mult)
+            engine = nc.vector if t == TILES - 1 else nc.gpsimd
+            engine.tensor_tensor(out=vp[:], in0=vp[:], in1=kb_of[t][:, h * CH:(h + 1) * CH], op=ALU.mult)
 
-        def side_sums(t):
-            for o in range(2):
-                nc.vector.scalar_tensor_tensor(
-                    out=side[t // 8][:, o, :], in0=vp_of[(t, 1)][:, CH - SPLIT:CH], scalar=wpad[t % NPAD][:, o:o + 1],
-                    in1=side[t // 8][:, o, :], op0=ALU.mult, op1=ALU.add,
-                )
+        def one_sum(force=False):
+            if queue and (force or ready_at[queue[0][0]] <= step[0]):
+                t, q = queue[0]
+                queue.remove((t, q))
+                if q < 0:
+                    moving_sum(t)
+                else:
+                    token_sum(t, q)
+                if queue and queue[0][0] // 8 == t // 8 or t % 8 != 7:
+                    return
+                if not [u for u, r in queue if u // 8 == t // 8]:
+                    finish(t // 8)
 
-        def token_sums(t, h):
+        def moving_sum(t):
             b, tt = divmod(t, 8)
             if tt == 0:
-                acc = sums.tile([P, CH], F32, name="sum%d" % h)
-                sum_of[h] = acc
-            width = CH - SPLIT if (h == 1 and t >= FIRST_SPLIT) else CH
-            nc.tensor.matmul(out=sum_of[h][:, 0:width], lhsT=wpad[t % NPAD][:], rhs=vp_of[(t, h)][:, 0:width], start=(tt == 0), stop=(tt == 7 and h == 0))
+                mv = sums.tile([P, CH], F32, name="mv")
+                mv_of[b] = mv
+            nc.tensor.matmul(out=mv_of[b][:, 0:MV], lhsT=wpad[t % NPAD][:], rhs=vp_of[(t, 0)][:, 0:MV], start=(tt == 0), stop=(tt == 7))
+
+        def token_sum(t, q):
+            b, tt = divmod(t, 8)
+            if b not in sum_of:
+                acc = sums.tile([P, 8, ST, 2], F32, name="st")
+                sum_of[b] = acc
+            h, lo = divmod(q * P, CH)
+            nc.tensor.matmul(out=sum_of[b][:, tt, q - (8 - ST), :], lhsT=vp_of[(t, h)][:, lo:lo + P], rhs=wpad[t % NPAD][:, 0:2], start=True, stop=True)
 
         def finish(b):
-            for o in range(2):
-                nc.tensor.matmul(out=sum_of[1][:, CH - SPLIT:CH], lhsT=pick[o][:], rhs=side[b][:, o, :], start=False, stop=(o == 1))
-            row = outs.tile([32, 2 * CH], F32, name="row")
-            for h in range(2):
-                nc.scalar.copy(out=row[:, h * CH:(h + 1) * CH], in_=sum_of[h][0:32, :])
-            nc.sync.dma_start(out=out_0[b], in_=row[0:1, :])
-            nc.sync.dma_start(out=out_1[b], in_=row[1:2, :])
+            tot = totals[b]
+            mrow = outs.tile([32, MV], F32, name="mrow")
+            if b == 0:
+                nc.scalar.copy(out=mrow[:], in_=mv_of[b][0:32, 0:MV])
+            nc.vector.tensor_reduce(out=tot[:, 0:2 * ST].rearrange("p (o q) -> p o q", o=2), in_=sum_of[b][:].rearrange("p t q o -> p o q t"), axis=AX.X, op=ALU.add)
+            if b == 1:
+                nc.scalar.copy(out=mrow[:], in_=mv_of[b][0:32, 0:MV])
+            nc.sync.dma_start(out=out_0[b][:, 0:MV], in_=mrow[0:1, :])
+            nc.scalar.dma_start(out=out_1[b][:, 0:MV], in_=mrow[1:2, :])
+            tp = mm.tile([P, CH], F32, name="ps")
+            nc.tensor.transpose(out=tp[:, 0:P], in_=tot[:], identity=ident[:])
+            row = outs.tile([32, P], F32, name="row")
+            nc.vector.tensor_copy(out=row[:], in_=tp[0:32, 0:P])
+            nc.sync.dma_start(out=out_0[b][:, MV:].rearrange("o (q m) -> (o q) m", m=P), in_=row[0:ST, :])
+            nc.scalar.dma_start(out=out_1[b][:, MV:].rearrange("o (q m) -> (o q) m", m=P), in_=row[ST:2 * ST, :])
 
         BANKS = sorted([(t, c) for t in range(TILES) for c in range(4)], key=arrival)
         first_use = {}
@@ -236,14 +265,14 @@ def tile_hydraattention_pa_kernel(tc, x, mask, W_kv, b_kv, out_0, out_1):
                 early_step[unit] = max(early_step[unit], quant_step[UNITS[k - NGRP]])
             quant_step[unit] = max(first_use[unit] - QUANT_LEAD, early_step[unit])
 
-        sums_at = {}
-        finish_at = {}
-        for n in range(len(BANKS) + R_LAG):
+        ORDER = [-1] + list(range(8 - ST, 8))
+        last = len(BANKS) + LAST_LAG
+        for n in range(last + 1):
+            step[0] = n
             if n == 0:
                 bias_copies()
                 for unit in UNITS[0:3]:
                     regroup(unit, "S")
-            if n == 0:
                 regroup(UNITS[0], "V")
                 quantise(UNITS[0], True)
                 regroup(UNITS[1], "V")
@@ -262,16 +291,14 @@ def tile_hydraattention_pa_kernel(tc, x, mask, W_kv, b_kv, out_0, out_1):
                 t, c = BANKS[n]
                 if c < 2:
                     keys(t, c)
+                    if c == 1:
+                        weights(t)
                 else:
                     values(t, c - 2)
                     if c == 3:
-                        sums_at[n + R_LAG] = t
-            if n in sums_at:
-                if sums_at[n] >= FIRST_SPLIT:
-                    side_sums(sums_at[n])
-                for h in range(2):
-                    token_sums(sums_at[n], h)
-                if sums_at[n] % 8 == 7:
-                    finish_at[min(n + F_LAG, len(BANKS) + R_LAG - 1)] = sums_at[n] // 8
-            if n in finish_at:
-                finish(finish_at[n])
+                        ready_at[t] = n + R_LAG
+                        for q in ORDER:
+                            queue.append((t, q))
+            if n >= last:
+                for k in range(len(queue)):
+                    one_sum(True)

@@ -19,15 +19,33 @@ PACK = 4
 G = 2
 CH = 512
 TILES = 16
-NGRP = 3
-UNITS = ['W0', 'X0', 'W1', 'W2', 'W3', 'X1', 'X2', 'X3']
-REGROUP = {'W0': 'VV', 'X0': 'SV', 'W1': 'SV', 'W2': 'SV', 'W3': 'SS', 'X1': 'SS', 'X2': 'SS', 'X3': 'SS'}
-R_LAG = 8
-NPAD = 6
-ST = 4
-MV = 1024 - 128 * ST
-JOBS = (1, 1)
+NGRP = 4
+UNITS = ['W0', 'X0', 'W2', 'W1', 'W3', 'X1', 'X2', 'X3']
+RL0 = 6
+RL1 = 6
+VP = (15,)
+FASTEND = 62
+LATE = 12
+LL0 = 3
+LL1 = 3
+FL = 0
+SEV = ()
+SIDE = tuple(range(16))
+NSIDE = 2
+LOW = 24
+S_LAG = 6
 LAST_LAG = 0
+HEADB = 4
+LOADS = [("W0", 0), ("X0", 0), ("W0", 1), ("X0", 1)]
+EV0 = [['V', 'W0', 0], ['V', 'X0', 0], ['B'], ['Q', 'W0', [0]], ['Q', 'X0', [0]], ['H'], ['V', 'W0', 1], ['S', 'X0', 1], ['Q', 'W0', [1]], ['M'], ['Q', 'X0', [1]]]
+GP = 4
+QL = 5
+RL = (12, 10)
+XENG = "SS"
+ASG = "..SVSVSSSS"
+PL = 6
+VL = 8
+WL = 7
 REGROUP_LEAD = 16
 QUANT_LEAD = 6
 RAWS = 8
@@ -64,15 +82,17 @@ def tile_hydraattention_pa_kernel(tc, x, mask, W_kv, b_kv, out_0, out_1):
 
         raw_of = {}
         for unit in UNITS:
-            idx = int(unit[1])
             raw = raws.tile([P, G, PACK, CH], BF16, name="raw")
-            for g in range(G):
+            raw_of[unit] = raw
+        for unit, g in LOADS + [(u, g) for u in UNITS for g in range(G) if (u, g) not in LOADS]:
+            idx = int(unit[1])
+            raw = raw_of[unit]
+            if True:
                 if unit[0] == "W":
                     src = wv[g][:, :, idx * CH:(idx + 1) * CH]
                 else:
                     src = xv[idx // 2, g][:, :, (idx % 2) * CH:(idx % 2 + 1) * CH]
                 nc.sync.dma_start(out=raw[:, g], in_=src)
-            raw_of[unit] = raw
 
         warm = const.tile([P, 1], F32, name="warm")
         nc.vector.memset(warm[:], 1.0)
@@ -87,11 +107,14 @@ def tile_hydraattention_pa_kernel(tc, x, mask, W_kv, b_kv, out_0, out_1):
         make_identity(nc, ident[:])
         ident16 = const.tile([P, P], BF16, name="ident16")
         make_identity(nc, ident16[:])
-        wpad = []
-        for k in range(NPAD):
-            wp = const.tile([P, P], F32, name="wpad%d" % k)
-            nc.gpsimd.memset(wp[:], 0.0)
-            wpad.append(wp)
+        pick = const.tile([P, 3], F32, name="pick")
+        nc.gpsimd.memset(pick[:], 0.0)
+        nc.gpsimd.memset(pick[:, 0:1], 1.0)
+        nc.gpsimd.memset(pick[:, 2:3], 1.0)
+        side = []
+        for b in range(2):
+            sd = const.tile([P, 2, NSIDE * P], F32, name="side%d" % b)
+            side.append(sd)
         totals = []
         for b in range(2):
             tot = const.tile([P, P], F32, name="tot%d" % b)
@@ -124,37 +147,47 @@ def tile_hydraattention_pa_kernel(tc, x, mask, W_kv, b_kv, out_0, out_1):
         kb_of = {}
         vp_of = {}
         sum_of = {}
-        mv_of = {}
+        w2_of = {}
         queue = []
         ready_at = {}
         step = [0]
+        weights_at = {}
+        WEIGHT_AT = {}
+        side_at = {}
+        acc_of = {}
 
-        def regroup(unit, engine, only=(0, 1)):
+        def regroup(unit, g, engine):
             if unit not in grp_of:
                 grp = grps.tile([P, G, CH, PACK], BF16, name="grp", align_bytes=64)
                 grp_of[unit] = grp
-            for g in only:
-                dst = grp_of[unit][:, g].rearrange("p (c i) t -> p c t i", i=4)
-                src = raw_of[unit][:, g].rearrange("p t (c i) -> p c t i", i=4)
-                if REGROUP[unit][g] == engine == "V":
-                    nc.vector.tensor_copy(out=dst, in_=src)
-                if REGROUP[unit][g] == "S" and engine == "S":
-                    nc.scalar.copy(out=dst, in_=src)
-                if REGROUP[unit][g] == "P" and engine == "S":
-                    for lo in range(0, CH, 256):
-                        ps2 = mm.tile([P, 4 * 256], BF16, name="ps")
-                        for q in range(2):
-                            rhs = raw_of[unit][:, g, :, lo + q * 128:lo + q * 128 + 128].rearrange("p t c -> p c t")
-                            nc.tensor.matmul(out=ps2[:, q * 512:(q + 1) * 512], lhsT=ident16[:], rhs=rhs, start=True, stop=True)
-                        nc.scalar.copy(out=grp_of[unit][:, g, lo:lo + 256].rearrange("p c t -> p (c t)"), in_=ps2[:])
+            dst = grp_of[unit][:, g].rearrange("p (c i) t -> p c t i", i=4)
+            src = raw_of[unit][:, g].rearrange("p t (c i) -> p c t i", i=4)
+            if engine == "V":
+                nc.vector.tensor_copy(out=dst, in_=src)
+            if engine == "S":
+                nc.scalar.copy(out=dst, in_=src)
+            if engine == "G":
+                for lo in range(0, CH // 4, CH // 4 // GP):
+                    hi = lo + CH // 4 // GP
+                    nc.gpsimd.tensor_scalar(out=dst[:, lo:hi], in0=src[:, lo:hi], scalar1=1.0, scalar2=0.0, op0=ALU.mult, op1=ALU.add)
+            if engine == "P":
+                for lo in range(0, CH, 256):
+                    ps2 = mm.tile([P, 4 * 256], BF16, name="ps")
+                    for q in range(2):
+                        rhs = raw_of[unit][:, g, :, lo + q * 128:lo + q * 128 + 128].rearrange("p t c -> p c t")
+                        nc.tensor.matmul(out=ps2[:, q * 512:(q + 1) * 512], lhsT=ident16[:], rhs=rhs, start=True, stop=True)
+                    nc.scalar.copy(out=grp_of[unit][:, g, lo:lo + 256].rearrange("p c t -> p (c t)"), in_=ps2[:])
 
-        def quantise(unit, halves):
-            cd = const.tile([P, G, CH], U32, name="cd_" + unit, align_bytes=64)
-            pl = const.tile([P, G, CH], U8, name="pl_" + unit, align_bytes=64)
-            codes[unit] = cd
-            planes[unit] = pl
-            if halves:
-                for g in range(G):
+        def quantise(unit, only):
+            if unit not in codes:
+                cd = const.tile([P, G, CH], U32, name="cd_" + unit, align_bytes=64)
+                pl = const.tile([P, G, CH], U8, name="pl_" + unit, align_bytes=64)
+                codes[unit] = cd
+                planes[unit] = pl
+            cd = codes[unit]
+            pl = planes[unit]
+            if len(only) == 1:
+                for g in only:
                     nc.vector.quantize_mx(
                         out=cd[:, g, :].bitcast(FP8X4),
                         scales=pl[:, g, :],
@@ -167,12 +200,15 @@ def tile_hydraattention_pa_kernel(tc, x, mask, W_kv, b_kv, out_0, out_1):
                     in_=grp_of[unit][:].rearrange("p g w t -> p (g w t)"),
                 )
 
-        def project(t, c, dst):
+        def one_pass(t, c, g):
             xu = "X%d" % (t // 4)
             wu = "W%d" % c
-            acc = mm.tile([P, CH], F32, name="ps")
+            if g == 0:
+                acc = mm.tile([P, CH], F32, name="ps")
+                acc_of[(t, c)] = acc
+            acc = acc_of[(t, c)]
             cols = slice((t % 4) * P, (t % 4 + 1) * P)
-            for g in range(G):
+            if True:
                 nc.tensor.matmul_mx(
                     out=acc[:],
                     lhsT=codes[xu][:, g, cols].bitcast(FP8X4),
@@ -182,9 +218,21 @@ def tile_hydraattention_pa_kernel(tc, x, mask, W_kv, b_kv, out_0, out_1):
                     start=(g == 0),
                     stop=(g == G - 1),
                 )
-                for k in range(JOBS[g]):
+
+        def project(t, c, dst):
+            for g in range(G):
+                if g == 0 and (t, c) in acc_of:
+                    continue
+                one_pass(t, c, g)
+                for k in range(2 if len(queue) > LOW or step[0] >= FASTEND else 1):
                     one_sum()
-            nc.vector.tensor_tensor(out=dst, in0=acc[:], in1=biasB[:, c * CH:(c + 1) * CH], op=ALU.add)
+            acc = acc_of[(t, c)]
+            bias = biasB[:, c * CH:(c + 1) * CH]
+            if (t, c) in SEV:
+                nc.scalar.copy(out=dst, in_=acc[:])
+                nc.gpsimd.tensor_tensor(out=dst, in0=dst, in1=bias, op=ALU.add)
+            else:
+                nc.vector.tensor_tensor(out=dst, in0=acc[:], in1=bias, op=ALU.add)
 
         def keys(t, h):
             if t not in kb_of:
@@ -198,107 +246,131 @@ def tile_hydraattention_pa_kernel(tc, x, mask, W_kv, b_kv, out_0, out_1):
             nc.scalar.activation(out=junk[:], in_=kb_of[t][:], func=ACT.Square, accum_out=n2[:])
             rn = const.tile([P, 1], F32, name="rn_%d" % t)
             nc.scalar.activation(out=rn[:], in_=n2[:], func=ACT.Abs_reciprocal_sqrt)
-            nc.scalar.activation(out=wpad[t % NPAD][:, 0:2], in_=mm2[:, t, :], func=ACT.Copy, scale=rn[:])
+            w2 = const.tile([P, 2], F32, name="w2_%d" % t)
+            w2_of[t] = w2
+            nc.scalar.activation(out=w2[:], in_=mm2[:, t, :], func=ACT.Copy, scale=rn[:])
 
         def values(t, h):
             vp = vps.tile([P, CH], F32, name="vp")
             vp_of[(t, h)] = vp
             project(t, 2 + h, vp[:])
-            engine = nc.vector if t == TILES - 1 else nc.gpsimd
+            engine = nc.vector if t in VP else nc.gpsimd
             engine.tensor_tensor(out=vp[:], in0=vp[:], in1=kb_of[t][:, h * CH:(h + 1) * CH], op=ALU.mult)
 
+        def has_side(t, q):
+            return t in SIDE and q >= 8 - NSIDE
+
         def one_sum(force=False):
-            if queue and (force or ready_at[queue[0][0]] <= step[0]):
+            if queue and (force or ready_at[queue[0]] <= step[0]):
                 t, q = queue[0]
                 queue.remove((t, q))
-                if q < 0:
-                    moving_sum(t)
-                else:
-                    token_sum(t, q)
-                if queue and queue[0][0] // 8 == t // 8 or t % 8 != 7:
-                    return
-                if not [u for u, r in queue if u // 8 == t // 8]:
+                token_sum(t, q)
+                if t % 8 == 7 and not [u for u, r in queue if u <= t]:
                     finish(t // 8)
 
-        def moving_sum(t):
+        def slot(t, q):
             b, tt = divmod(t, 8)
-            if tt == 0:
-                mv = sums.tile([P, CH], F32, name="mv")
-                mv_of[b] = mv
-            nc.tensor.matmul(out=mv_of[b][:, 0:MV], lhsT=wpad[t % NPAD][:], rhs=vp_of[(t, 0)][:, 0:MV], start=(tt == 0), stop=(tt == 7))
+            return len([u for u in range(8 * b, t) if not has_side(u, q)])
 
         def token_sum(t, q):
             b, tt = divmod(t, 8)
             if b not in sum_of:
-                acc = sums.tile([P, 8, ST, 2], F32, name="st")
+                acc = sums.tile([P, 9, 8, 2], F32, name="st%d" % b)
                 sum_of[b] = acc
+            if q >= 8:
+                nc.tensor.matmul(out=sum_of[b][:, slot(t + 1, q - 8), q - 8, :], lhsT=side[b][:, 0, (q - 16 + NSIDE) * P:(q - 15 + NSIDE) * P], rhs=pick[:, 0:2], start=True, stop=False)
+                nc.tensor.matmul(out=sum_of[b][:, slot(t + 1, q - 8), q - 8, :], lhsT=side[b][:, 1, (q - 16 + NSIDE) * P:(q - 15 + NSIDE) * P], rhs=pick[:, 1:3], start=False, stop=True)
+                return
             h, lo = divmod(q * P, CH)
-            nc.tensor.matmul(out=sum_of[b][:, tt, q - (8 - ST), :], lhsT=vp_of[(t, h)][:, lo:lo + P], rhs=wpad[t % NPAD][:, 0:2], start=True, stop=True)
+            nc.tensor.matmul(out=sum_of[b][:, slot(t, q), q, :], lhsT=vp_of[(t, h)][:, lo:lo + P], rhs=w2_of[t][:], start=True, stop=True)
+
+        def side_sums(t):
+            b = t // 8
+            first = not [u for u in SIDE if u // 8 == b and u < t]
+            for o in range(2):
+                src = vp_of[(t, 1)][:, CH - NSIDE * P:CH]
+                if first:
+                    nc.vector.tensor_scalar(out=side[b][:, o, :], in0=src, scalar1=w2_of[t][:, o:o + 1], scalar2=0.0, op0=ALU.mult, op1=ALU.add)
+                else:
+                    nc.vector.scalar_tensor_tensor(out=side[b][:, o, :], in0=src, scalar=w2_of[t][:, o:o + 1], in1=side[b][:, o, :], op0=ALU.mult, op1=ALU.add)
 
         def finish(b):
             tot = totals[b]
-            mrow = outs.tile([32, MV], F32, name="mrow")
-            if b == 0:
-                nc.scalar.copy(out=mrow[:], in_=mv_of[b][0:32, 0:MV])
-            nc.vector.tensor_reduce(out=tot[:, 0:2 * ST].rearrange("p (o q) -> p o q", o=2), in_=sum_of[b][:].rearrange("p t q o -> p o q t"), axis=AX.X, op=ALU.add)
-            if b == 1:
-                nc.scalar.copy(out=mrow[:], in_=mv_of[b][0:32, 0:MV])
-            nc.sync.dma_start(out=out_0[b][:, 0:MV], in_=mrow[0:1, :])
-            nc.scalar.dma_start(out=out_1[b][:, 0:MV], in_=mrow[1:2, :])
+            sided = [u for u in SIDE if u // 8 == b]
+            lo = 8 - NSIDE if sided else 8
+            t16 = tot[:, 0:16].rearrange("p (o q) -> p o q", o=2)
+            nc.vector.tensor_reduce(out=t16[:, :, 0:lo], in_=sum_of[b][:, 0:8, 0:lo, :].rearrange("p t q o -> p o q t"), axis=AX.X, op=ALU.add)
+            if lo < 8:
+                n = 9 - len(sided)
+                nc.vector.tensor_reduce(out=t16[:, :, lo:8], in_=sum_of[b][:, 0:n, lo:8, :].rearrange("p t q o -> p o q t"), axis=AX.X, op=ALU.add)
             tp = mm.tile([P, CH], F32, name="ps")
             nc.tensor.transpose(out=tp[:, 0:P], in_=tot[:], identity=ident[:])
             row = outs.tile([32, P], F32, name="row")
             nc.vector.tensor_copy(out=row[:], in_=tp[0:32, 0:P])
-            nc.sync.dma_start(out=out_0[b][:, MV:].rearrange("o (q m) -> (o q) m", m=P), in_=row[0:ST, :])
-            nc.scalar.dma_start(out=out_1[b][:, MV:].rearrange("o (q m) -> (o q) m", m=P), in_=row[ST:2 * ST, :])
+            nc.sync.dma_start(out=out_0[b].rearrange("o (q m) -> (o q) m", m=P), in_=row[0:8, :])
+            nc.scalar.dma_start(out=out_1[b].rearrange("o (q m) -> (o q) m", m=P), in_=row[8:16, :])
 
         BANKS = sorted([(t, c) for t in range(TILES) for c in range(4)], key=arrival)
         first_use = {}
         for n, (t, c) in enumerate(BANKS):
             for unit in ("X%d" % (t // 4), "W%d" % c):
                 first_use[unit] = min(first_use.get(unit, n), n)
-        early_step = {}
-        quant_step = {}
-        for k, unit in enumerate(UNITS):
-            early_step[unit] = max(first_use[unit] - REGROUP_LEAD, 0)
-            if k >= NGRP:
-                early_step[unit] = max(early_step[unit], quant_step[UNITS[k - NGRP]])
-            quant_step[unit] = max(first_use[unit] - QUANT_LEAD, early_step[unit])
-
-        ORDER = [-1] + list(range(8 - ST, 8))
         last = len(BANKS) + LAST_LAG
+        weight_step = {}
+        EV = {0: list(EV0)}
+        for k, unit in enumerate(UNITS[2:6]):
+            for g in range(2):
+                e = ASG[2 + 2 * k + g]
+                at = 0 if e in "SG" else max(first_use[unit] - (PL if e == "P" else VL), 0)
+                EV.setdefault(at, []).append([e, unit, g])
+        for unit in UNITS[2:]:
+            EV.setdefault(max(first_use[unit] - QL, 0), []).append(["Q", unit, [0, 1]])
+        for unit in UNITS[6:]:
+            for g in range(2):
+                EV.setdefault(first_use[unit] - RL[g], []).append([XENG[g], unit, g])
+        for t in range(TILES):
+            WEIGHT_AT[t] = WL if t < 4 else 0
         for n in range(last + 1):
             step[0] = n
-            if n == 0:
-                bias_copies()
-                for unit in UNITS[0:3]:
-                    regroup(unit, "S")
-                regroup(UNITS[0], "V")
-                quantise(UNITS[0], True)
-                regroup(UNITS[1], "V")
-                quantise(UNITS[1], True)
-                regroup(UNITS[2], "V")
-                mask_weights()
-                quantise(UNITS[2], False)
-            for unit in UNITS[3:]:
-                if early_step[unit] == n:
-                    regroup(unit, "S")
-                if quant_step[unit] == n + 1:
-                    regroup(unit, "V")
-                if quant_step[unit] == n:
-                    quantise(unit, False)
+            for ev in EV.get(n, ()):
+                if ev[0] == "B":
+                    bias_copies()
+                elif ev[0] == "M":
+                    mask_weights()
+                elif ev[0] == "H":
+                    for t, c in BANKS[0:HEADB]:
+                        one_pass(t, c, 0)
+                elif ev[0] == "Q":
+                    quantise(ev[1], ev[2])
+                else:
+                    regroup(ev[1], ev[2], ev[0])
+            for t in weights_at.get(n, ()):
+                weights(t)
+            for t in side_at.get(n, ()):
+                side_sums(t)
             if n < len(BANKS):
                 t, c = BANKS[n]
                 if c < 2:
                     keys(t, c)
                     if c == 1:
-                        weights(t)
+                        weights_at.setdefault(n + 1 + WEIGHT_AT.get(t, 0), []).append(t)
                 else:
                     values(t, c - 2)
                     if c == 3:
-                        ready_at[t] = n + R_LAG
-                        for q in ORDER:
-                            queue.append((t, q))
+                        if t % 8 == 7 and t not in SIDE and [u for u in SIDE if u // 8 == t // 8]:
+                            for q in range(8 - NSIDE, 8):
+                                ready_at[(t, q + 8)] = n + FL
+                                queue.append((t, q + 8))
+                        for q in range(8):
+                            if not has_side(t, q):
+                                ready_at[(t, q)] = n + ((RL1 if q > 3 else RL0) if t < LATE else (LL1 if q > 3 else LL0))
+                                queue.append((t, q))
+                        if t in SIDE:
+                            side_at.setdefault(min(n + S_LAG, last), []).append(t)
+                        if t % 8 == 7 and t in SIDE:
+                            for q in range(8 - NSIDE, 8):
+                                ready_at[(t, q + 8)] = n + max(RL1, S_LAG + 1)
+                                queue.append((t, q + 8))
             if n >= last:
                 for k in range(len(queue)):
                     one_sum(True)

@@ -35,16 +35,22 @@ NSIDE = 2
 LOW = 24
 S_LAG = 6
 LAST_LAG = 0
+MMB = 7
+CUTS = 2
+TURN = 3
+QX1 = 6
+HOLD = 2
+SL_LATE = 6
 HEADB = 4
 LOADS = [("W0", 0), ("X0", 0), ("W0", 1), ("X0", 1)]
-EV0 = [['V', 'W0', 0], ['V', 'X0', 0], ['B'], ['Q', 'W0', [0]], ['Q', 'X0', [0]], ['H'], ['V', 'W0', 1], ['S', 'X0', 1], ['Q', 'W0', [1]], ['M'], ['Q', 'X0', [1]]]
+EV0 = [['D'],['B'],['V', 'W0', 0], ['V', 'X0', 0],['Q', 'W0', [0]], ['Q', 'X0', [0]], ['H'], ['V', 'W0', 1], ['S', 'X0', 1], ['Q', 'W0', [1]], ['M'], ['Q', 'X0', [1]]]
 GP = 4
 QL = 5
 RL = (12, 10)
 XENG = "SS"
 ASG = "..SVSVSSSS"
 PL = 6
-VL = 8
+VL = 6
 WL = 7
 REGROUP_LEAD = 16
 QUANT_LEAD = 6
@@ -65,7 +71,7 @@ def tile_hydraattention_pa_kernel(tc, x, mask, W_kv, b_kv, out_0, out_1):
         kbs = ctx.enter_context(tc.tile_pool(name="kbs", bufs=6))
         vps = ctx.enter_context(tc.tile_pool(name="vps", bufs=12))
         junks = ctx.enter_context(tc.tile_pool(name="junks", bufs=2))
-        mm = ctx.enter_context(tc.psum_pool(name="mm", bufs=6))
+        mm = ctx.enter_context(tc.psum_pool(name="mm", bufs=MMB))
         sums = ctx.enter_context(tc.psum_pool(name="sums", bufs=1))
         outs = ctx.enter_context(tc.tile_pool(name="outs", bufs=4))
 
@@ -87,12 +93,14 @@ def tile_hydraattention_pa_kernel(tc, x, mask, W_kv, b_kv, out_0, out_1):
         for unit, g in LOADS + [(u, g) for u in UNITS for g in range(G) if (u, g) not in LOADS]:
             idx = int(unit[1])
             raw = raw_of[unit]
-            if True:
-                if unit[0] == "W":
-                    src = wv[g][:, :, idx * CH:(idx + 1) * CH]
-                else:
-                    src = xv[idx // 2, g][:, :, (idx % 2) * CH:(idx % 2 + 1) * CH]
-                nc.sync.dma_start(out=raw[:, g], in_=src)
+            if unit[0] == "W":
+                src = wv[g][:, :, idx * CH:(idx + 1) * CH]
+            else:
+                src = xv[idx // 2, g][:, :, (idx % 2) * CH:(idx % 2 + 1) * CH]
+            cuts = CUTS if (unit, g) == LOADS[0] else 1
+            for k in range(cuts):
+                piece = slice(k * CH // cuts, (k + 1) * CH // cuts)
+                nc.sync.dma_start(out=raw[:, g, :, piece], in_=src[:, :, piece])
 
         warm = const.tile([P, 1], F32, name="warm")
         nc.vector.memset(warm[:], 1.0)
@@ -100,7 +108,7 @@ def tile_hydraattention_pa_kernel(tc, x, mask, W_kv, b_kv, out_0, out_1):
         bias_row = const.tile([P, 4 * CH], BF16, name="bias_row")
         nc.vector.memset(bias_row[:], 0.0)
         mask_f = const.tile([P, P], F32, name="mask_f")
-        nc.vector.memset(mask_f[:], 0.0)
+        nc.gpsimd.memset(mask_f[:], 0.0)
         ones = const.tile([P, P], BF16, name="ones")
         nc.gpsimd.memset(ones[:], 1.0)
         ident = const.tile([P, P], F32, name="ident")
@@ -120,24 +128,26 @@ def tile_hydraattention_pa_kernel(tc, x, mask, W_kv, b_kv, out_0, out_1):
             tot = const.tile([P, P], F32, name="tot%d" % b)
             nc.gpsimd.memset(tot[:], 0.0)
             totals.append(tot)
-        nc.vector.tensor_copy(out=bias_row[0:1, :], in_=bias_in[:])
-        nc.vector.tensor_copy(out=mask_f[0:16, :], in_=mask_in[:])
+        nc.gpsimd.tensor_copy(out=mask_f[0:16, :], in_=mask_in[:])
 
         biasB = const.tile([P, 4 * CH], F32, name="biasB")
         bias_ps = []
-        for c in range(4):
-            ps = mm.tile([P, CH], F32, name="ps")
-            nc.tensor.matmul(out=ps[:], lhsT=ones[:], rhs=bias_row[:, c * CH:(c + 1) * CH], start=True, stop=True)
-            bias_ps.append(ps)
+
+        def bias_spread():
+            nc.vector.tensor_copy(out=bias_row[0:1, :], in_=bias_in[:])
+            for c in range(4):
+                ps = mm.tile([P, CH], F32, name="ps")
+                nc.tensor.matmul(out=ps[:], lhsT=ones[:], rhs=bias_row[:, c * CH:(c + 1) * CH], start=True, stop=True)
+                bias_ps.append(ps)
 
         def bias_copies():
             for c in range(4):
                 nc.scalar.copy(out=biasB[:, c * CH:(c + 1) * CH], in_=bias_ps[c][:])
-        ps = mm.tile([P, CH], F32, name="ps")
-        nc.tensor.transpose(out=ps[:, 0:P], in_=mask_f[:], identity=ident[:])
         mm2 = const.tile([P, TILES, 2], F32, name="mm2")
 
         def mask_weights():
+            ps = mm.tile([P, CH], F32, name="ps")
+            nc.tensor.transpose(out=ps[:, 0:P], in_=mask_f[:], identity=ident[:])
             nc.vector.tensor_scalar(out=mm2[:, :, 0], in0=ps[:, 0:TILES], scalar1=-1.0, scalar2=1.0, op0=ALU.mult, op1=ALU.add)
             nc.vector.tensor_copy(out=mm2[:, :, 1], in_=ps[:, 0:TILES])
 
@@ -155,15 +165,20 @@ def tile_hydraattention_pa_kernel(tc, x, mask, W_kv, b_kv, out_0, out_1):
         WEIGHT_AT = {}
         side_at = {}
         acc_of = {}
+        turn_at = []
+        hold = [0]
 
-        def regroup(unit, g, engine):
+        def regroup(unit, g, engine, part=None):
             if unit not in grp_of:
                 grp = grps.tile([P, G, CH, PACK], BF16, name="grp", align_bytes=64)
                 grp_of[unit] = grp
             dst = grp_of[unit][:, g].rearrange("p (c i) t -> p c t i", i=4)
             src = raw_of[unit][:, g].rearrange("p t (c i) -> p c t i", i=4)
             if engine == "V":
-                nc.vector.tensor_copy(out=dst, in_=src)
+                cuts = CUTS if (unit, g) == LOADS[0] else 1
+                for k in range(cuts) if part is None else [part]:
+                    piece = slice(k * CH // 4 // cuts, (k + 1) * CH // 4 // cuts)
+                    nc.vector.tensor_copy(out=dst[:, piece], in_=src[:, piece])
             if engine == "S":
                 nc.scalar.copy(out=dst, in_=src)
             if engine == "G":
@@ -263,6 +278,8 @@ def tile_hydraattention_pa_kernel(tc, x, mask, W_kv, b_kv, out_0, out_1):
         def one_sum(force=False):
             if queue and (force or ready_at[queue[0]] <= step[0]):
                 t, q = queue[0]
+                if t == 8 and step[0] < hold[0]:
+                    return
                 queue.remove((t, q))
                 token_sum(t, q)
                 if t % 8 == 7 and not [u for u, r in queue if u <= t]:
@@ -275,7 +292,7 @@ def tile_hydraattention_pa_kernel(tc, x, mask, W_kv, b_kv, out_0, out_1):
         def token_sum(t, q):
             b, tt = divmod(t, 8)
             if b not in sum_of:
-                acc = sums.tile([P, 9, 8, 2], F32, name="st%d" % b)
+                acc = sums.tile([P, 9, 8, 2], F32, name="st")
                 sum_of[b] = acc
             if q >= 8:
                 nc.tensor.matmul(out=sum_of[b][:, slot(t + 1, q - 8), q - 8, :], lhsT=side[b][:, 0, (q - 16 + NSIDE) * P:(q - 15 + NSIDE) * P], rhs=pick[:, 0:2], start=True, stop=False)
@@ -303,6 +320,14 @@ def tile_hydraattention_pa_kernel(tc, x, mask, W_kv, b_kv, out_0, out_1):
             if lo < 8:
                 n = 9 - len(sided)
                 nc.vector.tensor_reduce(out=t16[:, :, lo:8], in_=sum_of[b][:, 0:n, lo:8, :].rearrange("p t q o -> p o q t"), axis=AX.X, op=ALU.add)
+            if b == 0:
+                hold[0] = step[0] + HOLD
+                turn_at.append(step[0] + TURN)
+            else:
+                turn(b)
+
+        def turn(b):
+            tot = totals[b]
             tp = mm.tile([P, CH], F32, name="ps")
             nc.tensor.transpose(out=tp[:, 0:P], in_=tot[:], identity=ident[:])
             row = outs.tile([32, P], F32, name="row")
@@ -324,7 +349,7 @@ def tile_hydraattention_pa_kernel(tc, x, mask, W_kv, b_kv, out_0, out_1):
                 at = 0 if e in "SG" else max(first_use[unit] - (PL if e == "P" else VL), 0)
                 EV.setdefault(at, []).append([e, unit, g])
         for unit in UNITS[2:]:
-            EV.setdefault(max(first_use[unit] - QL, 0), []).append(["Q", unit, [0, 1]])
+            EV.setdefault(max(first_use[unit] - (QX1 if unit == "X1" else QL), 0), []).append(["Q", unit, [0, 1]])
         for unit in UNITS[6:]:
             for g in range(2):
                 EV.setdefault(first_use[unit] - RL[g], []).append([XENG[g], unit, g])
@@ -333,7 +358,9 @@ def tile_hydraattention_pa_kernel(tc, x, mask, W_kv, b_kv, out_0, out_1):
         for n in range(last + 1):
             step[0] = n
             for ev in EV.get(n, ()):
-                if ev[0] == "B":
+                if ev[0] == "D":
+                    bias_spread()
+                elif ev[0] == "B":
                     bias_copies()
                 elif ev[0] == "M":
                     mask_weights()
@@ -343,7 +370,9 @@ def tile_hydraattention_pa_kernel(tc, x, mask, W_kv, b_kv, out_0, out_1):
                 elif ev[0] == "Q":
                     quantise(ev[1], ev[2])
                 else:
-                    regroup(ev[1], ev[2], ev[0])
+                    regroup(ev[1], ev[2], ev[0], ev[3] if len(ev) > 3 else None)
+            if n in turn_at:
+                turn(0)
             for t in weights_at.get(n, ()):
                 weights(t)
             for t in side_at.get(n, ()):
@@ -366,7 +395,7 @@ def tile_hydraattention_pa_kernel(tc, x, mask, W_kv, b_kv, out_0, out_1):
                                 ready_at[(t, q)] = n + ((RL1 if q > 3 else RL0) if t < LATE else (LL1 if q > 3 else LL0))
                                 queue.append((t, q))
                         if t in SIDE:
-                            side_at.setdefault(min(n + S_LAG, last), []).append(t)
+                            side_at.setdefault(min(n + (S_LAG if t < 13 else SL_LATE), last), []).append(t)
                         if t % 8 == 7 and t in SIDE:
                             for q in range(8 - NSIDE, 8):
                                 ready_at[(t, q + 8)] = n + max(RL1, S_LAG + 1)

@@ -28,18 +28,18 @@ FASTEND = 62
 LATE = 12
 LL0 = 3
 LL1 = 3
-FL = 0
+FL = 1
 SEV = ()
 SIDE = tuple(range(16))
-NSIDE = 2
+NSIDE = (2, 2)
 LOW = 24
 S_LAG = 6
 LAST_LAG = 0
-MMB = 7
-CUTS = 2
+MMB = 6
+CUTS = 1
 TURN = 3
-QX1 = 6
-HOLD = 2
+QX1 = 5
+HOLD = 0
 SL_LATE = 6
 HEADB = 4
 LOADS = [("W0", 0), ("X0", 0), ("W0", 1), ("X0", 1)]
@@ -121,7 +121,7 @@ def tile_hydraattention_pa_kernel(tc, x, mask, W_kv, b_kv, out_0, out_1):
         nc.gpsimd.memset(pick[:, 2:3], 1.0)
         side = []
         for b in range(2):
-            sd = const.tile([P, 2, NSIDE * P], F32, name="side%d" % b)
+            sd = const.tile([P, 2, NSIDE[b] * P], F32, name="side%d" % b)
             side.append(sd)
         totals = []
         for b in range(2):
@@ -273,7 +273,7 @@ def tile_hydraattention_pa_kernel(tc, x, mask, W_kv, b_kv, out_0, out_1):
             engine.tensor_tensor(out=vp[:], in0=vp[:], in1=kb_of[t][:, h * CH:(h + 1) * CH], op=ALU.mult)
 
         def has_side(t, q):
-            return t in SIDE and q >= 8 - NSIDE
+            return t in SIDE and q >= 8 - NSIDE[t // 8]
 
         def one_sum(force=False):
             if queue and (force or ready_at[queue[0]] <= step[0]):
@@ -285,27 +285,28 @@ def tile_hydraattention_pa_kernel(tc, x, mask, W_kv, b_kv, out_0, out_1):
                 if t % 8 == 7 and not [u for u, r in queue if u <= t]:
                     finish(t // 8)
 
-        def slot(t, q):
-            b, tt = divmod(t, 8)
+        def slot(b, t, q):
             return len([u for u in range(8 * b, t) if not has_side(u, q)])
 
         def token_sum(t, q):
             b, tt = divmod(t, 8)
             if b not in sum_of:
-                acc = sums.tile([P, 9, 8, 2], F32, name="st")
+                acc = sums.tile([P, 9, 8, 2], F32, name="st%d" % b)
                 sum_of[b] = acc
             if q >= 8:
-                nc.tensor.matmul(out=sum_of[b][:, slot(t + 1, q - 8), q - 8, :], lhsT=side[b][:, 0, (q - 16 + NSIDE) * P:(q - 15 + NSIDE) * P], rhs=pick[:, 0:2], start=True, stop=False)
-                nc.tensor.matmul(out=sum_of[b][:, slot(t + 1, q - 8), q - 8, :], lhsT=side[b][:, 1, (q - 16 + NSIDE) * P:(q - 15 + NSIDE) * P], rhs=pick[:, 1:3], start=False, stop=True)
+                NSX = NSIDE[b]
+                nc.tensor.matmul(out=sum_of[b][:, slot(b, 8 * b + 8, q - 8), q - 8, :], lhsT=side[b][:, 0, (q - 16 + NSX) * P:(q - 15 + NSX) * P], rhs=pick[:, 0:2], start=True, stop=False)
+                nc.tensor.matmul(out=sum_of[b][:, slot(b, 8 * b + 8, q - 8), q - 8, :], lhsT=side[b][:, 1, (q - 16 + NSX) * P:(q - 15 + NSX) * P], rhs=pick[:, 1:3], start=False, stop=True)
                 return
             h, lo = divmod(q * P, CH)
-            nc.tensor.matmul(out=sum_of[b][:, slot(t, q), q, :], lhsT=vp_of[(t, h)][:, lo:lo + P], rhs=w2_of[t][:], start=True, stop=True)
+            nc.tensor.matmul(out=sum_of[b][:, slot(b, t, q), q, :], lhsT=vp_of[(t, h)][:, lo:lo + P], rhs=w2_of[t][:], start=True, stop=True)
 
         def side_sums(t):
             b = t // 8
+            NSX = NSIDE[b]
             first = not [u for u in SIDE if u // 8 == b and u < t]
             for o in range(2):
-                src = vp_of[(t, 1)][:, CH - NSIDE * P:CH]
+                src = vp_of[(t, 1)][:, CH - NSX * P:CH]
                 if first:
                     nc.vector.tensor_scalar(out=side[b][:, o, :], in0=src, scalar1=w2_of[t][:, o:o + 1], scalar2=0.0, op0=ALU.mult, op1=ALU.add)
                 else:
@@ -314,7 +315,7 @@ def tile_hydraattention_pa_kernel(tc, x, mask, W_kv, b_kv, out_0, out_1):
         def finish(b):
             tot = totals[b]
             sided = [u for u in SIDE if u // 8 == b]
-            lo = 8 - NSIDE if sided else 8
+            lo = 8 - NSIDE[b] if sided else 8
             t16 = tot[:, 0:16].rearrange("p (o q) -> p o q", o=2)
             nc.vector.tensor_reduce(out=t16[:, :, 0:lo], in_=sum_of[b][:, 0:8, 0:lo, :].rearrange("p t q o -> p o q t"), axis=AX.X, op=ALU.add)
             if lo < 8:
@@ -386,19 +387,15 @@ def tile_hydraattention_pa_kernel(tc, x, mask, W_kv, b_kv, out_0, out_1):
                 else:
                     values(t, c - 2)
                     if c == 3:
-                        if t % 8 == 7 and t not in SIDE and [u for u in SIDE if u // 8 == t // 8]:
-                            for q in range(8 - NSIDE, 8):
-                                ready_at[(t, q + 8)] = n + FL
-                                queue.append((t, q + 8))
                         for q in range(8):
                             if not has_side(t, q):
                                 ready_at[(t, q)] = n + ((RL1 if q > 3 else RL0) if t < LATE else (LL1 if q > 3 else LL0))
                                 queue.append((t, q))
                         if t in SIDE:
                             side_at.setdefault(min(n + (S_LAG if t < 13 else SL_LATE), last), []).append(t)
-                        if t % 8 == 7 and t in SIDE:
-                            for q in range(8 - NSIDE, 8):
-                                ready_at[(t, q + 8)] = n + max(RL1, S_LAG + 1)
+                        if t in SIDE and not [u for u in SIDE if u // 8 == t // 8 and u > t]:
+                            for q in range(8 - NSIDE[t // 8], 8):
+                                ready_at[(t, q + 8)] = n + (S_LAG if t < 13 else SL_LATE) + FL
                                 queue.append((t, q + 8))
             if n >= last:
                 for k in range(len(queue)):

from contextlib import ExitStack

import concourse.mybir as mybir
from concourse.masks import make_identity

FLOPS = 2 * 2048 * 1024 * 2048

F32 = mybir.dt.float32
BF16 = mybir.dt.bfloat16
U32 = mybir.dt.uint32
U8 = mybir.dt.uint8
FP8X4 = mybir.dt.float8_e4m3fn_x4
ALU = mybir.AluOpType
ACT = mybir.ActivationFunctionType
AX = mybir.AxisListType

P = 128
PACK = 4
G = 2
CH = 512
TILES = 16
NGRP = 4
UNITS = ['W0', 'X0', 'W2', 'W1', 'W3', 'X1', 'X2', 'X3']
RL0 = 6
RL1 = 6
VP = (15,)
FASTEND = 62
LATE = 12
LL0 = 3
LL1 = 3
FL = 1
SEV = ()
SIDE = tuple(range(16))
NSIDE = (2, 2)
LOW = 24
S_LAG = 6
LAST_LAG = 0
MMB = 6
CUTS = 1
TURN = 3
QX1 = 5
HOLD = 0
SL_LATE = 6
HEADB = 4
LOADS = [("W0", 0), ("X0", 0), ("W0", 1), ("X0", 1)]
EV0 = [['D'],['B'],['V', 'W0', 0], ['V', 'X0', 0],['Q', 'W0', [0]], ['Q', 'X0', [0]], ['H'], ['V', 'W0', 1], ['S', 'X0', 1], ['Q', 'W0', [1]], ['M'], ['Q', 'X0', [1]]]
GP = 4
QL = 5
RL = (12, 10)
XENG = "SS"
ASG = "..SVSVSSSS"
PL = 6
VL = 6
WL = 7
REGROUP_LEAD = 16
QUANT_LEAD = 6
RAWS = 8


def arrival(bank):
    return max(UNITS.index("X%d" % (bank[0] // 4)), UNITS.index("W%d" % bank[1]))


def tile_hydraattention_pa_kernel(tc, x, mask, W_kv, b_kv, out_0, out_1):
    nc = tc.nc
    with ExitStack() as ctx:
        ctx.enter_context(tc.manual_schedule())
        const = ctx.enter_context(tc.tile_pool(name="const", bufs=1))
        raws = ctx.enter_context(tc.tile_pool(name="raws", bufs=RAWS))
        grps = ctx.enter_context(tc.tile_pool(name="grps", bufs=NGRP))
        kbs = ctx.enter_context(tc.tile_pool(name="kbs", bufs=6))
        vps = ctx.enter_context(tc.tile_pool(name="vps", bufs=12))
        junks = ctx.enter_context(tc.tile_pool(name="junks", bufs=2))
        mm = ctx.enter_context(tc.psum_pool(name="mm", bufs=MMB))
        sums = ctx.enter_context(tc.psum_pool(name="sums", bufs=1))
        outs = ctx.enter_context(tc.tile_pool(name="outs", bufs=4))

        xv = x.rearrange("b (g p j) h w -> b g p j (h w)", g=G, p=P, j=PACK)
        wv = W_kv.rearrange("(g p j) n -> g p j n", g=G, p=P, j=PACK)

        bias_in = const.tile([1, 4 * CH], BF16, name="bias_in")
        nc.scalar.dma_start(out=bias_in[:], in_=b_kv.rearrange("(o n) -> o n", o=1))
        mask_in = const.tile([16, P], BF16, name="mask_in")
        nc.scalar.dma_start(
            out=mask_in[:],
            in_=mask.rearrange("b o h w -> (b o h w)").rearrange("(r c) -> r c", c=P),
        )

        raw_of = {}
        for unit in UNITS:
            raw = raws.tile([P, G, PACK, CH], BF16, name="raw")
            raw_of[unit] = raw
        for unit, g in LOADS + [(u, g) for u in UNITS for g in range(G) if (u, g) not in LOADS]:
            idx = int(unit[1])
            raw = raw_of[unit]
            if unit[0] == "W":
                src = wv[g][:, :, idx * CH:(idx + 1) * CH]
            else:
                src = xv[idx // 2, g][:, :, (idx % 2) * CH:(idx % 2 + 1) * CH]
            cuts = CUTS if (unit, g) == LOADS[0] else 1
            for k in range(cuts):
                piece = slice(k * CH // cuts, (k + 1) * CH // cuts)
                nc.sync.dma_start(out=raw[:, g, :, piece], in_=src[:, :, piece])

        warm = const.tile([P, 1], F32, name="warm")
        nc.vector.memset(warm[:], 1.0)
        nc.scalar.activation(out=warm[:], in_=warm[:], func=ACT.Abs_reciprocal_sqrt)
        bias_row = const.tile([P, 4 * CH], BF16, name="bias_row")
        nc.vector.memset(bias_row[:], 0.0)
        mask_f = const.tile([P, P], F32, name="mask_f")
        nc.gpsimd.memset(mask_f[:], 0.0)
        ones = const.tile([P, P], BF16, name="ones")
        nc.gpsimd.memset(ones[:], 1.0)
        ident = const.tile([P, P], F32, name="ident")
        make_identity(nc, ident[:])
        ident16 = const.tile([P, P], BF16, name="ident16")
        make_identity(nc, ident16[:])
        pick = const.tile([P, 3], F32, name="pick")
        nc.gpsimd.memset(pick[:], 0.0)
        nc.gpsimd.memset(pick[:, 0:1], 1.0)
        nc.gpsimd.memset(pick[:, 2:3], 1.0)
        side = []
        for b in range(2):
            sd = const.tile([P, 2, NSIDE[b] * P], F32, name="side%d" % b)
            side.append(sd)
        totals = []
        for b in range(2):
            tot = const.tile([P, P], F32, name="tot%d" % b)
            nc.gpsimd.memset(tot[:], 0.0)
            totals.append(tot)
        nc.gpsimd.tensor_copy(out=mask_f[0:16, :], in_=mask_in[:])

        biasB = const.tile([P, 4 * CH], F32, name="biasB")
        bias_ps = []

        def bias_spread():
            nc.vector.tensor_copy(out=bias_row[0:1, :], in_=bias_in[:])
            for c in range(4):
                ps = mm.tile([P, CH], F32, name="ps")
                nc.tensor.matmul(out=ps[:], lhsT=ones[:], rhs=bias_row[:, c * CH:(c + 1) * CH], start=True, stop=True)
                bias_ps.append(ps)

        def bias_copies():
            for c in range(4):
                nc.scalar.copy(out=biasB[:, c * CH:(c + 1) * CH], in_=bias_ps[c][:])
        mm2 = const.tile([P, TILES, 2], F32, name="mm2")

        def mask_weights():
            ps = mm.tile([P, CH], F32, name="ps")
            nc.tensor.transpose(out=ps[:, 0:P], in_=mask_f[:], identity=ident[:])
            nc.vector.tensor_scalar(out=mm2[:, :, 0], in0=ps[:, 0:TILES], scalar1=-1.0, scalar2=1.0, op0=ALU.mult, op1=ALU.add)
            nc.vector.tensor_copy(out=mm2[:, :, 1], in_=ps[:, 0:TILES])

        grp_of = {}
        codes = {}
        planes = {}
        kb_of = {}
        vp_of = {}
        sum_of = {}
        w2_of = {}
        queue = []
        ready_at = {}
        step = [0]
        weights_at = {}
        WEIGHT_AT = {}
        side_at = {}
        acc_of = {}
        turn_at = []
        hold = [0]

        def regroup(unit, g, engine, part=None):
            if unit not in grp_of:
                grp = grps.tile([P, G, CH, PACK], BF16, name="grp", align_bytes=64)
                grp_of[unit] = grp
            dst = grp_of[unit][:, g].rearrange("p (c i) t -> p c t i", i=4)
            src = raw_of[unit][:, g].rearrange("p t (c i) -> p c t i", i=4)
            if engine == "V":
                cuts = CUTS if (unit, g) == LOADS[0] else 1
                for k in range(cuts) if part is None else [part]:
                    piece = slice(k * CH // 4 // cuts, (k + 1) * CH // 4 // cuts)
                    nc.vector.tensor_copy(out=dst[:, piece], in_=src[:, piece])
            if engine == "S":
                nc.scalar.copy(out=dst, in_=src)
            if engine == "G":
                for lo in range(0, CH // 4, CH // 4 // GP):
                    hi = lo + CH // 4 // GP
                    nc.gpsimd.tensor_scalar(out=dst[:, lo:hi], in0=src[:, lo:hi], scalar1=1.0, scalar2=0.0, op0=ALU.mult, op1=ALU.add)
            if engine == "P":
                for lo in range(0, CH, 256):
                    ps2 = mm.tile([P, 4 * 256], BF16, name="ps")
                    for q in range(2):
                        rhs = raw_of[unit][:, g, :, lo + q * 128:lo + q * 128 + 128].rearrange("p t c -> p c t")
                        nc.tensor.matmul(out=ps2[:, q * 512:(q + 1) * 512], lhsT=ident16[:], rhs=rhs, start=True, stop=True)
                    nc.scalar.copy(out=grp_of[unit][:, g, lo:lo + 256].rearrange("p c t -> p (c t)"), in_=ps2[:])

        def quantise(unit, only):
            if unit not in codes:
                cd = const.tile([P, G, CH], U32, name="cd_" + unit, align_bytes=64)
                pl = const.tile([P, G, CH], U8, name="pl_" + unit, align_bytes=64)
                codes[unit] = cd
                planes[unit] = pl
            cd = codes[unit]
            pl = planes[unit]
            if len(only) == 1:
                for g in only:
                    nc.vector.quantize_mx(
                        out=cd[:, g, :].bitcast(FP8X4),
                        scales=pl[:, g, :],
                        in_=grp_of[unit][:, g].rearrange("p w t -> p (w t)"),
                    )
            else:
                nc.vector.quantize_mx(
                    out=cd[:].rearrange("p g w -> p (g w)").bitcast(FP8X4),
                    scales=pl[:].rearrange("p g w -> p (g w)"),
                    in_=grp_of[unit][:].rearrange("p g w t -> p (g w t)"),
                )

        def one_pass(t, c, g):
            xu = "X%d" % (t // 4)
            wu = "W%d" % c
            if g == 0:
                acc = mm.tile([P, CH], F32, name="ps")
                acc_of[(t, c)] = acc
            acc = acc_of[(t, c)]
            cols = slice((t % 4) * P, (t % 4 + 1) * P)
            if True:
                nc.tensor.matmul_mx(
                    out=acc[:],
                    lhsT=codes[xu][:, g, cols].bitcast(FP8X4),
                    lhsT_scale=planes[xu][:, g, cols],
                    rhs=codes[wu][:, g, :].bitcast(FP8X4),
                    rhs_scale=planes[wu][:, g, :],
                    start=(g == 0),
                    stop=(g == G - 1),
                )

        def project(t, c, dst):
            for g in range(G):
                if g == 0 and (t, c) in acc_of:
                    continue
                one_pass(t, c, g)
                for k in range(2 if len(queue) > LOW or step[0] >= FASTEND else 1):
                    one_sum()
            acc = acc_of[(t, c)]
            bias = biasB[:, c * CH:(c + 1) * CH]
            if (t, c) in SEV:
                nc.scalar.copy(out=dst, in_=acc[:])
                nc.gpsimd.tensor_tensor(out=dst, in0=dst, in1=bias, op=ALU.add)
            else:
                nc.vector.tensor_tensor(out=dst, in0=acc[:], in1=bias, op=ALU.add)

        def keys(t, h):
            if t not in kb_of:
                kb = kbs.tile([P, 2 * CH], F32, name="kb")
                kb_of[t] = kb
            project(t, h, kb_of[t][:, h * CH:(h + 1) * CH])

        def weights(t):
            n2 = const.tile([P, 1], F32, name="n2_%d" % t)
            junk = junks.tile([P, 2 * CH], BF16, name="junk")
            nc.scalar.activation(out=junk[:], in_=kb_of[t][:], func=ACT.Square, accum_out=n2[:])
            rn = const.tile([P, 1], F32, name="rn_%d" % t)
            nc.scalar.activation(out=rn[:], in_=n2[:], func=ACT.Abs_reciprocal_sqrt)
            w2 = const.tile([P, 2], F32, name="w2_%d" % t)
            w2_of[t] = w2
            nc.scalar.activation(out=w2[:], in_=mm2[:, t, :], func=ACT.Copy, scale=rn[:])

        def values(t, h):
            vp = vps.tile([P, CH], F32, name="vp")
            vp_of[(t, h)] = vp
            project(t, 2 + h, vp[:])
            engine = nc.vector if t in VP else nc.gpsimd
            engine.tensor_tensor(out=vp[:], in0=vp[:], in1=kb_of[t][:, h * CH:(h + 1) * CH], op=ALU.mult)

        def has_side(t, q):
            return t in SIDE and q >= 8 - NSIDE[t // 8]

        def one_sum(force=False):
            if queue and (force or ready_at[queue[0]] <= step[0]):
                t, q = queue[0]
                if t == 8 and step[0] < hold[0]:
                    return
                queue.remove((t, q))
                token_sum(t, q)
                if t % 8 == 7 and not [u for u, r in queue if u <= t]:
                    finish(t // 8)

        def slot(b, t, q):
            return len([u for u in range(8 * b, t) if not has_side(u, q)])

        def token_sum(t, q):
            b, tt = divmod(t, 8)
            if b not in sum_of:
                acc = sums.tile([P, 9, 8, 2], F32, name="st%d" % b)
                sum_of[b] = acc
            if q >= 8:
                NSX = NSIDE[b]
                nc.tensor.matmul(out=sum_of[b][:, slot(b, 8 * b + 8, q - 8), q - 8, :], lhsT=side[b][:, 0, (q - 16 + NSX) * P:(q - 15 + NSX) * P], rhs=pick[:, 0:2], start=True, stop=False)
                nc.tensor.matmul(out=sum_of[b][:, slot(b, 8 * b + 8, q - 8), q - 8, :], lhsT=side[b][:, 1, (q - 16 + NSX) * P:(q - 15 + NSX) * P], rhs=pick[:, 1:3], start=False, stop=True)
                return
            h, lo = divmod(q * P, CH)
            nc.tensor.matmul(out=sum_of[b][:, slot(b, t, q), q, :], lhsT=vp_of[(t, h)][:, lo:lo + P], rhs=w2_of[t][:], start=True, stop=True)

        def side_sums(t):
            b = t // 8
            NSX = NSIDE[b]
            first = not [u for u in SIDE if u // 8 == b and u < t]
            for o in range(2):
                src = vp_of[(t, 1)][:, CH - NSX * P:CH]
                if first:
                    nc.vector.tensor_scalar(out=side[b][:, o, :], in0=src, scalar1=w2_of[t][:, o:o + 1], scalar2=0.0, op0=ALU.mult, op1=ALU.add)
                else:
                    nc.vector.scalar_tensor_tensor(out=side[b][:, o, :], in0=src, scalar=w2_of[t][:, o:o + 1], in1=side[b][:, o, :], op0=ALU.mult, op1=ALU.add)

        def finish(b):
            tot = totals[b]
            sided = [u for u in SIDE if u // 8 == b]
            lo = 8 - NSIDE[b] if sided else 8
            t16 = tot[:, 0:16].rearrange("p (o q) -> p o q", o=2)
            nc.vector.tensor_reduce(out=t16[:, :, 0:lo], in_=sum_of[b][:, 0:8, 0:lo, :].rearrange("p t q o -> p o q t"), axis=AX.X, op=ALU.add)
            if lo < 8:
                n = 9 - len(sided)
                nc.vector.tensor_reduce(out=t16[:, :, lo:8], in_=sum_of[b][:, 0:n, lo:8, :].rearrange("p t q o -> p o q t"), axis=AX.X, op=ALU.add)
            if b == 0:
                hold[0] = step[0] + HOLD
                turn_at.append(step[0] + TURN)
            else:
                turn(b)

        def turn(b):
            tot = totals[b]
            tp = mm.tile([P, CH], F32, name="ps")
            nc.tensor.transpose(out=tp[:, 0:P], in_=tot[:], identity=ident[:])
            row = outs.tile([32, P], F32, name="row")
            nc.vector.tensor_copy(out=row[:], in_=tp[0:32, 0:P])
            nc.sync.dma_start(out=out_0[b].rearrange("o (q m) -> (o q) m", m=P), in_=row[0:8, :])
            nc.scalar.dma_start(out=out_1[b].rearrange("o (q m) -> (o q) m", m=P), in_=row[8:16, :])

        BANKS = sorted([(t, c) for t in range(TILES) for c in range(4)], key=arrival)
        first_use = {}
        for n, (t, c) in enumerate(BANKS):
            for unit in ("X%d" % (t // 4), "W%d" % c):
                first_use[unit] = min(first_use.get(unit, n), n)
        last = len(BANKS) + LAST_LAG
        weight_step = {}
        EV = {0: list(EV0)}
        for k, unit in enumerate(UNITS[2:6]):
            for g in range(2):
                e = ASG[2 + 2 * k + g]
                at = 0 if e in "SG" else max(first_use[unit] - (PL if e == "P" else VL), 0)
                EV.setdefault(at, []).append([e, unit, g])
        for unit in UNITS[2:]:
            EV.setdefault(max(first_use[unit] - (QX1 if unit == "X1" else QL), 0), []).append(["Q", unit, [0, 1]])
        for unit in UNITS[6:]:
            for g in range(2):
                EV.setdefault(first_use[unit] - RL[g], []).append([XENG[g], unit, g])
        for t in range(TILES):
            WEIGHT_AT[t] = WL if t < 4 else 0
        for n in range(last + 1):
            step[0] = n
            for ev in EV.get(n, ()):
                if ev[0] == "D":
                    bias_spread()
                elif ev[0] == "B":
                    bias_copies()
                elif ev[0] == "M":
                    mask_weights()
                elif ev[0] == "H":
                    for t, c in BANKS[0:HEADB]:
                        one_pass(t, c, 0)
                elif ev[0] == "Q":
                    quantise(ev[1], ev[2])
                else:
                    regroup(ev[1], ev[2], ev[0], ev[3] if len(ev) > 3 else None)
            if n in turn_at:
                turn(0)
            for t in weights_at.get(n, ()):
                weights(t)
            for t in side_at.get(n, ()):
                side_sums(t)
            if n < len(BANKS):
                t, c = BANKS[n]
                if c < 2:
                    keys(t, c)
                    if c == 1:
                        weights_at.setdefault(n + 1 + WEIGHT_AT.get(t, 0), []).append(t)
                else:
                    values(t, c - 2)
                    if c == 3:
                        for q in range(8):
                            if not has_side(t, q):
                                ready_at[(t, q)] = n + ((RL1 if q > 3 else RL0) if t < LATE else (LL1 if q > 3 else LL0))
                                queue.append((t, q))
                        if t in SIDE:
                            side_at.setdefault(min(n + (S_LAG if t < 13 else SL_LATE), last), []).append(t)
                        if t in SIDE and not [u for u in SIDE if u // 8 == t // 8 and u > t]:
                            for q in range(8 - NSIDE[t // 8], 8):
                                ready_at[(t, q + 8)] = n + (S_LAG if t < 13 else SL_LATE) + FL
                                queue.append((t, q + 8))
            if n >= last:
                for k in range(len(queue)):
                    one_sum(True)
